import numpy as np
import ml_dtypes


def mxq(x, axis, fmt="e4m3"):
    dtype, down = {"e4m3": (ml_dtypes.float8_e4m3fn, 7), "e5m2": (ml_dtypes.float8_e5m2, 14)}[fmt]
    v = np.moveaxis(np.asarray(x, np.float32).astype(ml_dtypes.bfloat16).astype(np.float64), axis, -1)
    blocks = v.reshape(v.shape[:-1] + (-1, 32))
    amax = np.abs(blocks).max(-1, keepdims=True)
    byte = np.maximum(np.where(amax > 0, np.frexp(amax)[1] - 1 + 127, 0) - down, 1)
    scale = np.exp2(byte - 127.0)
    codes = (blocks / scale).astype(np.float32).astype(dtype).astype(np.float64)
    return np.moveaxis((codes * scale).reshape(v.shape), -1, axis)


WIDE = False


def mx_kscale(k):
    if not WIDE:
        return np.ones(k)
    levels = np.array([10, -10, 5, -5, 0])
    a = np.random.permutation(np.resize(levels, k // 512 * 4)).reshape(k // 512, 4)
    idx = np.arange(k)
    return np.exp2(a[idx // 512, idx % 128 // 32])


BF16 = ml_dtypes.bfloat16


def bf(x):
    return np.asarray(x, np.float32).astype(BF16)


def f64(x):
    return np.asarray(x).astype(np.float64)


E2M1 = np.array([0.0, 0.5, 1.0, 1.5, 2.0, 3.0, 4.0, 6.0, -0.0, -0.5, -1.0, -1.5, -2.0, -3.0, -4.0, -6.0])


def pack_weight(w, fmt):
    k, n = w.shape
    w = f64(bf(w)).reshape(k // 32, 32, n)
    amax = np.abs(w).max(1)
    if fmt == "e4m3":
        byte = np.frexp(amax)[1] - 1 + 127 - 7
    else:
        mant, ex = np.frexp(amax / 6.0)
        byte = np.where(mant > 0.5, ex, ex - 1) + 127
    byte = np.clip(np.where(amax > 0, byte, 1), 1, 254)
    scaled = (w * np.exp2(127.0 - byte)[:, None, :]).reshape(k, n).astype(np.float32)
    by_word = np.ascontiguousarray(scaled.reshape(k // 512, 128, 4, n).transpose(0, 1, 3, 2))
    if fmt == "e4m3":
        words = by_word.astype(ml_dtypes.float8_e4m3fn).view(np.uint8)
    else:
        c = by_word.astype(ml_dtypes.float4_e2m1fn).view(np.uint8) & 0xF
        words = c[..., 0::2] | (c[..., 1::2] << 4)
    return np.ascontiguousarray(words), np.ascontiguousarray(byte.astype(np.uint8).reshape(k // 512, 16, n))


def unpack_weight(words, scales, fmt):
    g, p, n, _ = words.shape
    if fmt == "e4m3":
        vals = np.ascontiguousarray(words).view(ml_dtypes.float8_e4m3fn).astype(np.float64)
    else:
        nib = np.empty((g, p, n, 4), np.uint8)
        nib[..., 0::2] = words & 0xF
        nib[..., 1::2] = words >> 4
        vals = E2M1[nib]
    vals = vals * np.repeat(np.exp2(scales.astype(np.float64) - 127.0), 8, axis=1)[..., None]
    return vals.transpose(0, 1, 3, 2).reshape(g * 512, n)

def pack4(w):
    words, scales = pack_weight(w, "e2m1")
    return words.reshape(words.shape[0], 128, -1), scales


def unpack4(words, scales):
    return unpack_weight(words.reshape(words.shape[0], 128, -1, 2), scales, "e2m1")


B, HW, C, HID, WS, SS, HEADS = 1, 32, 1024, 2048, 8, 4, 16
L = HW * HW
NH = HW // WS
EPS = 1e-5


def adain(x, scale, shift):
    m = x.mean(2, keepdims=True)
    s = np.std(x, axis=2, keepdims=True, ddof=1) + EPS
    return (x - m) / s * scale + shift


def setup_inputs():
    s = mx_kscale(C)
    o_attn = bf(0.4 * np.random.standard_normal((NH * NH * B, WS * WS, C)) * s)
    out_w = np.random.standard_normal((C, C)) / np.sqrt(C) / s[None, :]
    words, scales = pack4(np.ascontiguousarray(out_w.T))
    return {"o_attn": o_attn,
            "out_w_words": words,
            "out_w_scales": scales,
            "out_b": bf(0.1 * np.random.standard_normal(C)),
            "ada1_scale": bf(1.0 + 0.1 * np.random.standard_normal((1, L, 1))),
            "ada1_shift": bf(0.1 * np.random.standard_normal((1, L, 1))),
            "x": bf(np.random.standard_normal((B, L, C)))}


def reference(o_attn, out_w_words, out_w_scales, out_b, ada1_scale, ada1_shift, x):
    a = (mxq(f64(o_attn), 2, "e4m3") @ unpack4(out_w_words, out_w_scales)) + f64(out_b)
    a = np.swapaxes(a.reshape(B, NH, NH, WS, WS, C), 2, 3).reshape(B, HW, HW, C)
    a = np.roll(a, (SS, SS), axis=(1, 2)).reshape(B, L, C)
    return f64(x) + adain(a, f64(ada1_scale), f64(ada1_shift))

@@ -1,0 +1,263 @@
+from contextlib import ExitStack
+
+import concourse.mybir as mybir
+from concourse.masks import make_identity
+
+F32 = mybir.dt.float32
+BF16 = mybir.dt.bfloat16
+I32 = mybir.dt.int32
+U32 = mybir.dt.uint32
+U8 = mybir.dt.uint8
+FP8X4 = mybir.dt.float8_e4m3fn_x4
+FP4X4 = mybir.dt.float4_e2m1fn_x4
+ALU = mybir.AluOpType
+ACT = mybir.ActivationFunctionType
+
+P = 128
+C = 1024
+TOKENS = 1024
+N_TILES = TOKENS // P
+PACK = 4
+K_PASS = P * PACK
+PASSES = C // K_PASS
+BANK = 512
+HALVES = C // BANK
+WINDOWS_IN_ROW = 4
+WINDOW = 8
+GRID = 32
+SHIFT = 4
+ROWS_IN_TILE = P // GRID
+EPS = 1e-5
+
+FLOPS = 2 * TOKENS * C * C
+
+
+def tile_swintransformerblock_pb_kernel(
+    tc, o_attn, out_w_words, out_w_scales, out_b, ada1_scale, ada1_shift, x, out
+):
+    nc = tc.nc
+    with ExitStack() as ctx:
+        keep = ctx.enter_context(tc.tile_pool(name="keep", bufs=1))
+        per_tile = ctx.enter_context(tc.tile_pool(name="per_tile", bufs=N_TILES))
+        psum_t = ctx.enter_context(tc.psum_pool(name="psum_t", bufs=2))
+        psum_a = ctx.enter_context(tc.psum_pool(name="psum_a", bufs=3))
+        ctx.enter_context(tc.manual_schedule())
+
+        bias_rows = keep.tile([P, C], BF16, name="bias_rows")
+        w_planes = keep.tile([P, PASSES, C], U8, name="w_planes", align_bytes=64)
+        token_rows = keep.tile([P, P], BF16, name="token_rows")
+        ones = keep.tile([P, P], BF16, name="ones")
+        nc.vector.memset(bias_rows[:], 0.0)
+        nc.vector.memset(w_planes[:].rearrange("p g n -> p (g n)").bitcast(I32), 0)
+        nc.vector.memset(token_rows[:], 0.0)
+        nc.vector.memset(ones[:], 1.0)
+
+        identity = keep.tile([P, P], F32, name="identity")
+        make_identity(nc, identity[:])
+
+        nc.scalar.dma_start(out=bias_rows[0:1, :], in_=out_b.rearrange("(o c) -> o c", o=1))
+        nc.scalar.dma_start(
+            out=token_rows[0:N_TILES, :],
+            in_=ada1_scale.rearrange("o (t p) i -> (o t) (p i)", p=P),
+        )
+        nc.scalar.dma_start(
+            out=token_rows[N_TILES : 2 * N_TILES, :],
+            in_=ada1_shift.rearrange("o (t p) i -> (o t) (p i)", p=P),
+        )
+        table_warmer = keep.tile([P, 1], F32, name="table_warmer")
+        nc.scalar.activation(out=table_warmer[:], in_=ones[:, 0:1], func=ACT.Sqrt)
+
+        def first_token(n):
+            return ((n + SHIFT // ROWS_IN_TILE) % N_TILES) * P
+
+        attention = [per_tile.tile([P, C], BF16, name="attention", tag="attention") for n in range(N_TILES)]
+        residual = [per_tile.tile([P, C], BF16, name="residual", tag="residual") for n in range(N_TILES)]
+
+        def load_attention(n):
+            band, half = divmod(n, WINDOW // ROWS_IN_TILE)
+            places = GRID * half
+            nc.sync.dma_start(
+                out=attention[n][:],
+                in_=o_attn[
+                    WINDOWS_IN_ROW * band : WINDOWS_IN_ROW * (band + 1), places : places + GRID, :
+                ].rearrange("w q c -> q w c"),
+            )
+
+        load_attention(0)
+        for quadrant in range(4):
+            nc.sync.dma_start(
+                out=w_planes[32 * quadrant : 32 * quadrant + 4, :, :].bitcast(I32),
+                in_=out_w_scales[:, 4 * quadrant : 4 * quadrant + 4, :].rearrange("g r n -> r g n").bitcast(I32),
+            )
+        w_words = keep.tile([P, PASSES, 2 * C], U8, name="w_words", align_bytes=64)
+        for g in range(PASSES):
+            nc.sync.dma_start(out=w_words[:, g, :].bitcast(I32), in_=out_w_words[g].bitcast(I32))
+        for n in range(1, N_TILES):
+            load_attention(n)
+        for n in range(N_TILES):
+            nc.sync.dma_start(out=residual[n][:], in_=x[0, first_token(n) : first_token(n) + P, :])
+
+        permutation = keep.tile([P, P], F32, name="permutation")
+        from_partition = identity[:].rearrange("p (d c w) -> p d w c", d=ROWS_IN_TILE, c=WINDOW, w=WINDOWS_IN_ROW)
+        to_column = permutation[:].rearrange("p (d j) -> p d j", d=ROWS_IN_TILE)
+        last = WINDOWS_IN_ROW - 1
+        nc.vector.tensor_copy(
+            out=to_column[:, :, SHIFT : SHIFT + last * WINDOW].rearrange("p d (w c) -> p d w c", w=last),
+            in_=from_partition[:, :, 0:last, :],
+        )
+        nc.vector.tensor_copy(out=to_column[:, :, GRID - SHIFT : GRID], in_=from_partition[:, :, last, 0:SHIFT])
+        nc.vector.tensor_copy(out=to_column[:, :, 0:SHIFT], in_=from_partition[:, :, last, SHIFT:WINDOW])
+
+        transposed = {}
+        grouped = {}
+        codes = {}
+        planes = {}
+        product = {}
+        biased = {}
+        neg_mean = {}
+        deviation = {}
+        gain = {}
+        offset = {}
+        result = {}
+
+        def transpose(n):
+            transposed[n] = psum_t.tile([P, PASSES, 2, P], F32, name="transposed", tag="transposed")
+            pairs = attention[n][:].bitcast(F32)
+            for g in range(PASSES):
+                for u in range(2):
+                    nc.tensor.transpose(
+                        transposed[n][:, g, u, :],
+                        pairs[:, (K_PASS // 2) * g + u : (K_PASS // 2) * (g + 1) : 2],
+                        permutation[:],
+                    )
+
+        def copy_out(n):
+            grouped[n] = per_tile.tile([P, PASSES, P, PACK], BF16, name="grouped", tag="grouped", align_bytes=64)
+            nc.scalar.copy(out=grouped[n][:].bitcast(F32), in_=transposed[n][:].rearrange("p g u m -> p g m u"))
+
+        def quantise(n):
+            codes[n] = per_tile.tile([P, PASSES * P], U32, name="codes", tag="codes", align_bytes=64)
+            planes[n] = per_tile.tile([P, PASSES * P], U8, name="planes", tag="planes", align_bytes=64)
+            nc.vector.quantize_mx(
+                out=codes[n][:].bitcast(FP8X4),
+                scales=planes[n][:],
+                in_=grouped[n][:].rearrange("p g m t -> p (g m t)"),
+            )
+
+        def project(n):
+            product[n] = psum_a.tile([P, HALVES, BANK], F32, name="product", tag="product")
+            for h in range(HALVES):
+                for g in range(PASSES):
+                    nc.tensor.matmul_mx(
+                        out=product[n][:, h, :],
+                        lhsT=codes[n][:, P * g : P * (g + 1)].bitcast(FP8X4),
+                        lhsT_scale=planes[n][:, P * g : P * (g + 1)],
+                        rhs=w_words[:, g, 2 * BANK * h : 2 * BANK * (h + 1)].bitcast(FP4X4),
+                        rhs_scale=w_planes[:, g, BANK * h : BANK * (h + 1)],
+                        start=(g == 0),
+                        stop=(g == PASSES - 1),
+                    )
+
+        def add_bias(n):
+            biased[n] = per_tile.tile([P, C], F32, name="biased", tag="biased")
+            sums = per_tile.tile([P, HALVES], F32, name="sums", tag="sums")
+            for h in range(HALVES):
+                nc.vector.scalar_tensor_tensor(
+                    out=biased[n][:, BANK * h : BANK * (h + 1)],
+                    in0=product[n][:, h, :],
+                    scalar=1.0,
+                    in1=bias_all[:, BANK * h : BANK * (h + 1)],
+                    op0=ALU.mult,
+                    op1=ALU.add,
+                    accum_out=sums[:, h : h + 1],
+                )
+            neg_mean[n] = per_tile.tile([P, 1], F32, name="neg_mean", tag="neg_mean")
+            nc.vector.tensor_scalar(
+                out=neg_mean[n][:],
+                in0=sums[:, 0:1],
+                scalar1=sums[:, 1:2],
+                scalar2=-1.0 / C,
+                op0=ALU.add,
+                op1=ALU.mult,
+            )
+
+        def measure(n):
+            squares = per_tile.tile([P, C], BF16, name="squares", tag="squares")
+            sum_squares = per_tile.tile([P, 1], F32, name="sum_squares", tag="sum_squares")
+            nc.scalar.activation(
+                out=squares[:], in_=biased[n][:], func=ACT.Square, bias=neg_mean[n][:], accum_out=sum_squares[:]
+            )
+            deviation[n] = per_tile.tile([P, 1], F32, name="deviation", tag="deviation")
+            nc.scalar.activation(out=deviation[n][:], in_=sum_squares[:], func=ACT.Sqrt, scale=1.0 / (C - 1))
+
+        def fold(n):
+            t = first_token(n) // P
+            padded = per_tile.tile([P, 1], F32, name="padded", tag="padded")
+            inverse = per_tile.tile([P, 1], F32, name="inverse", tag="inverse")
+            gain[n] = per_tile.tile([P, 1], F32, name="gain", tag="gain")
+            offset[n] = per_tile.tile([P, 1], F32, name="offset", tag="offset")
+            nc.vector.tensor_scalar_add(out=padded[:], in0=deviation[n][:], scalar1=EPS)
+            nc.vector.reciprocal(out=inverse[:], in_=padded[:])
+            nc.vector.tensor_mul(out=gain[n][:], in0=inverse[:], in1=token_columns[:, t : t + 1])
+            nc.vector.scalar_tensor_tensor(
+                out=offset[n][:],
+                in0=neg_mean[n][:],
+                scalar=gain[n][:],
+                in1=token_columns[:, N_TILES + t : N_TILES + t + 1],
+                op0=ALU.mult,
+                op1=ALU.add,
+            )
+
+        def normalise(n):
+            result[n] = per_tile.tile([P, C], F32, name="result", tag="result")
+            nc.scalar.activation(
+                out=result[n][:], in_=biased[n][:], func=ACT.Identity, scale=gain[n][:], bias=offset[n][:]
+            )
+
+        def add_residual_and_store(n):
+            nc.vector.tensor_add(out=result[n][:], in0=result[n][:], in1=residual[n][:])
+            nc.sync.dma_start(out=out[0, first_token(n) : first_token(n) + P, :], in_=result[n][:])
+
+        transpose(0)
+        copy_out(0)
+        transpose(1)
+
+        bias_bank = psum_a.tile([P, HALVES, BANK], F32, name="bias_bank", tag="product")
+        bias_all = keep.tile([P, C], F32, name="bias_all")
+        for h in range(HALVES):
+            nc.tensor.matmul(
+                out=bias_bank[:, h, :], lhsT=ones[:], rhs=bias_rows[:, BANK * h : BANK * (h + 1)], start=True, stop=True
+            )
+            nc.scalar.copy(out=bias_all[:, BANK * h : BANK * (h + 1)], in_=bias_bank[:, h, :])
+
+        quantise(0)
+        project(0)
+
+        token_rows_f32 = keep.tile([P, P], F32, name="token_rows_f32")
+        token_bank = psum_t.tile([P, P], F32, name="token_bank", tag="transposed")
+        token_columns = keep.tile([P, 2 * N_TILES], F32, name="token_columns")
+        nc.vector.tensor_copy(out=token_rows_f32[:], in_=token_rows[:])
+        nc.tensor.transpose(token_bank[:], token_rows_f32[:], identity[:])
+        nc.vector.tensor_copy(out=token_columns[:], in_=token_bank[:, 0 : 2 * N_TILES])
+
+        def live(n):
+            return 0 <= n < N_TILES
+
+        for step in range(-1, N_TILES + 2):
+            if live(step + 2):
+                copy_out(step + 2)
+            if live(step + 3):
+                transpose(step + 3)
+            if live(step):
+                add_bias(step)
+            if live(step + 2):
+                quantise(step + 2)
+                project(step + 2)
+            if live(step - 2):
+                normalise(step - 2)
+            if live(step - 1):
+                fold(step - 1)
+            if live(step):
+                measure(step)
+            if live(step - 2):
+                add_residual_and_store(step - 2)

@@ -51,19 +51,13 @@ def tile_swintransformerblock_pb_kernel(
         nc.vector.memset(w_planes[:].rearrange("p g n -> p (g n)").bitcast(I32), 0)
         nc.vector.memset(token_rows[:], 0.0)
         nc.vector.memset(ones[:], 1.0)
+        minus_one = keep.tile([P, 1], F32, name="minus_one")
+        nc.vector.memset(minus_one[:], -1.0)
 
         identity = keep.tile([P, P], F32, name="identity")
         make_identity(nc, identity[:])
 
         nc.scalar.dma_start(out=bias_rows[0:1, :], in_=out_b.rearrange("(o c) -> o c", o=1))
-        nc.scalar.dma_start(
-            out=token_rows[0:N_TILES, :],
-            in_=ada1_scale.rearrange("o (t p) i -> (o t) (p i)", p=P),
-        )
-        nc.scalar.dma_start(
-            out=token_rows[N_TILES : 2 * N_TILES, :],
-            in_=ada1_shift.rearrange("o (t p) i -> (o t) (p i)", p=P),
-        )
         table_warmer = keep.tile([P, 1], F32, name="table_warmer")
         nc.scalar.activation(out=table_warmer[:], in_=ones[:, 0:1], func=ACT.Sqrt)
 
@@ -71,7 +65,7 @@ def tile_swintransformerblock_pb_kernel(
             return ((n + SHIFT // ROWS_IN_TILE) % N_TILES) * P
 
         attention = [per_tile.tile([P, C], BF16, name="attention", tag="attention") for n in range(N_TILES)]
-        residual = [per_tile.tile([P, C], BF16, name="residual", tag="residual") for n in range(N_TILES)]
+        residual = keep.tile([P, N_TILES, C], BF16, name="residual")
 
         def load_attention(n):
             band, half = divmod(n, WINDOW // ROWS_IN_TILE)
@@ -84,18 +78,25 @@ def tile_swintransformerblock_pb_kernel(
             )
 
         load_attention(0)
+        w_words = keep.tile([P, PASSES, 2 * C], U8, name="w_words", align_bytes=64)
+        nc.sync.dma_start(out=w_words[:].bitcast(I32), in_=out_w_words.rearrange("g p b -> p g b").bitcast(I32))
         for quadrant in range(4):
             nc.sync.dma_start(
                 out=w_planes[32 * quadrant : 32 * quadrant + 4, :, :].bitcast(I32),
                 in_=out_w_scales[:, 4 * quadrant : 4 * quadrant + 4, :].rearrange("g r n -> r g n").bitcast(I32),
             )
-        w_words = keep.tile([P, PASSES, 2 * C], U8, name="w_words", align_bytes=64)
-        for g in range(PASSES):
-            nc.sync.dma_start(out=w_words[:, g, :].bitcast(I32), in_=out_w_words[g].bitcast(I32))
-        for n in range(1, N_TILES):
+        for n in range(1, N_TILES // 2):
             load_attention(n)
-        for n in range(N_TILES):
-            nc.sync.dma_start(out=residual[n][:], in_=x[0, first_token(n) : first_token(n) + P, :])
+        nc.sync.dma_start(out=token_rows[0:N_TILES, :], in_=ada1_scale.rearrange("o (t p) i -> (o t) (p i)", p=P))
+        nc.sync.dma_start(
+            out=token_rows[N_TILES : 2 * N_TILES, :], in_=ada1_shift.rearrange("o (t p) i -> (o t) (p i)", p=P)
+        )
+        for n in range(N_TILES // 2, N_TILES):
+            load_attention(n)
+        for t in range(0, N_TILES, 2):
+            nc.sync.dma_start(
+                out=residual[:, t : t + 2, :], in_=x[0, P * t : P * (t + 2), :].rearrange("(t p) c -> p t c", p=P)
+            )
 
         permutation = keep.tile([P, P], F32, name="permutation")
         from_partition = identity[:].rearrange("p (d c w) -> p d w c", d=ROWS_IN_TILE, c=WINDOW, w=WINDOWS_IN_ROW)
@@ -114,7 +115,9 @@ def tile_swintransformerblock_pb_kernel(
         planes = {}
         product = {}
         biased = {}
+        sums = {}
         neg_mean = {}
+        sum_squares = {}
         deviation = {}
         gain = {}
         offset = {}
@@ -160,7 +163,7 @@ def tile_swintransformerblock_pb_kernel(
 
         def add_bias(n):
             biased[n] = per_tile.tile([P, C], F32, name="biased", tag="biased")
-            sums = per_tile.tile([P, HALVES], F32, name="sums", tag="sums")
+            sums[n] = per_tile.tile([P, HALVES], F32, name="sums", tag="sums")
             for h in range(HALVES):
                 nc.vector.scalar_tensor_tensor(
                     out=biased[n][:, BANK * h : BANK * (h + 1)],
@@ -169,26 +172,30 @@ def tile_swintransformerblock_pb_kernel(
                     in1=bias_all[:, BANK * h : BANK * (h + 1)],
                     op0=ALU.mult,
                     op1=ALU.add,
-                    accum_out=sums[:, h : h + 1],
+                    accum_out=sums[n][:, h : h + 1],
                 )
+
+        def mean(n):
             neg_mean[n] = per_tile.tile([P, 1], F32, name="neg_mean", tag="neg_mean")
-            nc.vector.tensor_scalar(
+            nc.gpsimd.tensor_scalar(
                 out=neg_mean[n][:],
-                in0=sums[:, 0:1],
-                scalar1=sums[:, 1:2],
+                in0=sums[n][:, 0:1],
+                scalar1=sums[n][:, 1:2],
                 scalar2=-1.0 / C,
                 op0=ALU.add,
                 op1=ALU.mult,
             )
 
-        def measure(n):
+        def square(n):
             squares = per_tile.tile([P, C], BF16, name="squares", tag="squares")
-            sum_squares = per_tile.tile([P, 1], F32, name="sum_squares", tag="sum_squares")
+            sum_squares[n] = per_tile.tile([P, 1], F32, name="sum_squares", tag="sum_squares")
             nc.scalar.activation(
-                out=squares[:], in_=biased[n][:], func=ACT.Square, bias=neg_mean[n][:], accum_out=sum_squares[:]
+                out=squares[:], in_=biased[n][:], func=ACT.Square, bias=neg_mean[n][:], accum_out=sum_squares[n][:]
             )
+
+        def root(n):
             deviation[n] = per_tile.tile([P, 1], F32, name="deviation", tag="deviation")
-            nc.scalar.activation(out=deviation[n][:], in_=sum_squares[:], func=ACT.Sqrt, scale=1.0 / (C - 1))
+            nc.scalar.activation(out=deviation[n][:], in_=sum_squares[n][:], func=ACT.Sqrt, scale=1.0 / (C - 1))
 
         def fold(n):
             t = first_token(n) // P
@@ -196,14 +203,16 @@ def tile_swintransformerblock_pb_kernel(
             inverse = per_tile.tile([P, 1], F32, name="inverse", tag="inverse")
             gain[n] = per_tile.tile([P, 1], F32, name="gain", tag="gain")
             offset[n] = per_tile.tile([P, 1], F32, name="offset", tag="offset")
-            nc.vector.tensor_scalar_add(out=padded[:], in0=deviation[n][:], scalar1=EPS)
-            nc.vector.reciprocal(out=inverse[:], in_=padded[:])
-            nc.vector.tensor_mul(out=gain[n][:], in0=inverse[:], in1=token_columns[:, t : t + 1])
-            nc.vector.scalar_tensor_tensor(
+            nc.gpsimd.tensor_scalar(
+                out=padded[:], in0=deviation[n][:], scalar1=1.0, scalar2=EPS, op0=ALU.mult, op1=ALU.add
+            )
+            nc.gpsimd.tensor_tensor(out=inverse[:], in0=padded[:], in1=minus_one[:], op=ALU.pow)
+            nc.gpsimd.tensor_tensor(out=gain[n][:], in0=inverse[:], in1=token_columns[:, t : t + 1], op=ALU.mult)
+            nc.gpsimd.tensor_scalar(
                 out=offset[n][:],
                 in0=neg_mean[n][:],
-                scalar=gain[n][:],
-                in1=token_columns[:, N_TILES + t : N_TILES + t + 1],
+                scalar1=gain[n][:],
+                scalar2=token_columns[:, N_TILES + t : N_TILES + t + 1],
                 op0=ALU.mult,
                 op1=ALU.add,
             )
@@ -215,49 +224,58 @@ def tile_swintransformerblock_pb_kernel(
             )
 
         def add_residual_and_store(n):
-            nc.vector.tensor_add(out=result[n][:], in0=result[n][:], in1=residual[n][:])
+            nc.vector.tensor_add(out=result[n][:], in0=result[n][:], in1=residual[:, first_token(n) // P, :])
             nc.sync.dma_start(out=out[0, first_token(n) : first_token(n) + P, :], in_=result[n][:])
-
-        transpose(0)
-        copy_out(0)
-        transpose(1)
 
         bias_bank = psum_a.tile([P, HALVES, BANK], F32, name="bias_bank", tag="product")
         bias_all = keep.tile([P, C], F32, name="bias_all")
+        transpose(0)
+        copy_out(0)
+        transpose(1)
         for h in range(HALVES):
             nc.tensor.matmul(
                 out=bias_bank[:, h, :], lhsT=ones[:], rhs=bias_rows[:, BANK * h : BANK * (h + 1)], start=True, stop=True
             )
-            nc.scalar.copy(out=bias_all[:, BANK * h : BANK * (h + 1)], in_=bias_bank[:, h, :])
-
         quantise(0)
         project(0)
+        copy_out(1)
+        nc.vector.tensor_copy(out=bias_all[:, 0:BANK], in_=bias_bank[:, 0, :])
+        nc.scalar.copy(out=bias_all[:, BANK:C], in_=bias_bank[:, 1, :])
+        transpose(2)
+        quantise(1)
+        project(1)
 
         token_rows_f32 = keep.tile([P, P], F32, name="token_rows_f32")
-        token_bank = psum_t.tile([P, P], F32, name="token_bank", tag="transposed")
         token_columns = keep.tile([P, 2 * N_TILES], F32, name="token_columns")
-        nc.vector.tensor_copy(out=token_rows_f32[:], in_=token_rows[:])
-        nc.tensor.transpose(token_bank[:], token_rows_f32[:], identity[:])
-        nc.vector.tensor_copy(out=token_columns[:], in_=token_bank[:, 0 : 2 * N_TILES])
+
+        def spread_token_vectors():
+            token_bank = psum_t.tile([P, P], F32, name="token_bank", tag="transposed")
+            nc.gpsimd.tensor_copy(out=token_rows_f32[:], in_=token_rows[:])
+            nc.tensor.transpose(token_bank[:], token_rows_f32[:], identity[:])
+            nc.scalar.copy(out=token_columns[:], in_=token_bank[:, 0 : 2 * N_TILES])
 
         def live(n):
             return 0 <= n < N_TILES
 
-        for step in range(-1, N_TILES + 2):
-            if live(step + 2):
-                copy_out(step + 2)
+        for step in range(N_TILES + 4):
+            if live(step - 1):
+                square(step - 1)
             if live(step + 3):
                 transpose(step + 3)
             if live(step):
                 add_bias(step)
+                mean(step)
+            if live(step + 2):
+                copy_out(step + 2)
+            if live(step - 1):
+                root(step - 1)
+                fold(step - 1)
+            if live(step - 3):
+                add_residual_and_store(step - 3)
             if live(step + 2):
                 quantise(step + 2)
                 project(step + 2)
+            if step == 0:
+                spread_token_vectors()
             if live(step - 2):
                 normalise(step - 2)
-            if live(step - 1):
-                fold(step - 1)
-            if live(step):
-                measure(step)
-            if live(step - 2):
-                add_residual_and_store(step - 2)

@@ -28,6 +28,8 @@ GRID = 32
 SHIFT = 4
 ROWS_IN_TILE = P // GRID
 EPS = 1e-5
+GROUP = N_TILES // 2
+VECTOR_TILES = 2
 
 FLOPS = 2 * TOKENS * C * C
 
@@ -47,11 +49,13 @@ def tile_swintransformerblock_pb_kernel(
         w_planes = keep.tile([P, PASSES, C], U8, name="w_planes", align_bytes=64)
         token_rows = keep.tile([P, P], BF16, name="token_rows")
         ones = keep.tile([P, P], BF16, name="ones")
+        one_half = keep.tile([P, GROUP], F32, name="one_half")
+        minus_one = keep.tile([P, GROUP], F32, name="minus_one")
         nc.vector.memset(bias_rows[:], 0.0)
         nc.vector.memset(w_planes[:].rearrange("p g n -> p (g n)").bitcast(I32), 0)
         nc.vector.memset(token_rows[:], 0.0)
         nc.vector.memset(ones[:], 1.0)
-        minus_one = keep.tile([P, 1], F32, name="minus_one")
+        nc.vector.memset(one_half[:], 0.5)
         nc.vector.memset(minus_one[:], -1.0)
 
         identity = keep.tile([P, P], F32, name="identity")
@@ -59,21 +63,18 @@ def tile_swintransformerblock_pb_kernel(
 
         nc.scalar.dma_start(out=bias_rows[0:1, :], in_=out_b.rearrange("(o c) -> o c", o=1))
         table_warmer = keep.tile([P, 1], F32, name="table_warmer")
-        nc.scalar.activation(out=table_warmer[:], in_=ones[:, 0:1], func=ACT.Sqrt)
+        nc.scalar.activation(out=table_warmer[:], in_=ones[:, 0:1], func=ACT.Square)
 
-        def first_token(n):
-            return ((n + SHIFT // ROWS_IN_TILE) % N_TILES) * P
-
-        attention = [per_tile.tile([P, C], BF16, name="attention", tag="attention") for n in range(N_TILES)]
+        attention = [per_tile.tile([P, C], BF16, name="attention", tag="attention") for t in range(N_TILES)]
         residual = keep.tile([P, N_TILES, C], BF16, name="residual")
 
-        def load_attention(n):
-            band, half = divmod(n, WINDOW // ROWS_IN_TILE)
-            places = GRID * half
+        def load_attention(t):
+            band, window_row = divmod((ROWS_IN_TILE * t - SHIFT) % GRID, WINDOW)
+            places = WINDOW * window_row
             nc.sync.dma_start(
-                out=attention[n][:],
+                out=attention[t][:],
                 in_=o_attn[
-                    WINDOWS_IN_ROW * band : WINDOWS_IN_ROW * (band + 1), places : places + GRID, :
+                    WINDOWS_IN_ROW * band : WINDOWS_IN_ROW * (band + 1), places : places + ROWS_IN_TILE * WINDOW, :
                 ].rearrange("w q c -> q w c"),
             )
 
@@ -85,14 +86,12 @@ def tile_swintransformerblock_pb_kernel(
                 out=w_planes[32 * quadrant : 32 * quadrant + 4, :, :].bitcast(I32),
                 in_=out_w_scales[:, 4 * quadrant : 4 * quadrant + 4, :].rearrange("g r n -> r g n").bitcast(I32),
             )
-        for n in range(1, N_TILES // 2):
-            load_attention(n)
+        for t in range(1, N_TILES):
+            load_attention(t)
         nc.sync.dma_start(out=token_rows[0:N_TILES, :], in_=ada1_scale.rearrange("o (t p) i -> (o t) (p i)", p=P))
         nc.sync.dma_start(
             out=token_rows[N_TILES : 2 * N_TILES, :], in_=ada1_shift.rearrange("o (t p) i -> (o t) (p i)", p=P)
         )
-        for n in range(N_TILES // 2, N_TILES):
-            load_attention(n)
         for t in range(0, N_TILES, 2):
             nc.sync.dma_start(
                 out=residual[:, t : t + 2, :], in_=x[0, P * t : P * (t + 2), :].rearrange("(t p) c -> p t c", p=P)
@@ -115,117 +114,123 @@ def tile_swintransformerblock_pb_kernel(
         planes = {}
         product = {}
         biased = {}
-        sums = {}
-        neg_mean = {}
-        sum_squares = {}
-        deviation = {}
-        gain = {}
-        offset = {}
         result = {}
+        sums = keep.tile([P, N_TILES, HALVES], F32, name="sums")
+        neg_mean = keep.tile([P, N_TILES], F32, name="neg_mean")
+        sum_squares = keep.tile([P, N_TILES], F32, name="sum_squares")
+        root = keep.tile([P, N_TILES], F32, name="root")
+        padded = keep.tile([P, N_TILES], F32, name="padded")
+        inverse = keep.tile([P, N_TILES], F32, name="inverse")
+        gain = keep.tile([P, N_TILES], F32, name="gain")
+        mean_gain = keep.tile([P, N_TILES], F32, name="mean_gain")
+        offset = keep.tile([P, N_TILES], F32, name="offset")
 
-        def transpose(n):
-            transposed[n] = psum_t.tile([P, PASSES, 2, P], F32, name="transposed", tag="transposed")
-            pairs = attention[n][:].bitcast(F32)
+        def transpose(t):
+            transposed[t] = psum_t.tile([P, PASSES, 2, P], F32, name="transposed", tag="transposed")
+            pairs = attention[t][:].bitcast(F32)
             for g in range(PASSES):
                 for u in range(2):
                     nc.tensor.transpose(
-                        transposed[n][:, g, u, :],
+                        transposed[t][:, g, u, :],
                         pairs[:, (K_PASS // 2) * g + u : (K_PASS // 2) * (g + 1) : 2],
                         permutation[:],
                     )
 
-        def copy_out(n):
-            grouped[n] = per_tile.tile([P, PASSES, P, PACK], BF16, name="grouped", tag="grouped", align_bytes=64)
-            nc.scalar.copy(out=grouped[n][:].bitcast(F32), in_=transposed[n][:].rearrange("p g u m -> p g m u"))
+        def copy_out(t):
+            grouped[t] = per_tile.tile([P, PASSES, P, PACK], BF16, name="grouped", tag="grouped", align_bytes=64)
+            nc.scalar.copy(out=grouped[t][:].bitcast(F32), in_=transposed[t][:].rearrange("p g u m -> p g m u"))
 
-        def quantise(n):
-            codes[n] = per_tile.tile([P, PASSES * P], U32, name="codes", tag="codes", align_bytes=64)
-            planes[n] = per_tile.tile([P, PASSES * P], U8, name="planes", tag="planes", align_bytes=64)
+        def quantise(t):
+            codes[t] = per_tile.tile([P, PASSES * P], U32, name="codes", tag="codes", align_bytes=64)
+            planes[t] = per_tile.tile([P, PASSES * P], U8, name="planes", tag="planes", align_bytes=64)
             nc.vector.quantize_mx(
-                out=codes[n][:].bitcast(FP8X4),
-                scales=planes[n][:],
-                in_=grouped[n][:].rearrange("p g m t -> p (g m t)"),
+                out=codes[t][:].bitcast(FP8X4),
+                scales=planes[t][:],
+                in_=grouped[t][:].rearrange("p g m i -> p (g m i)"),
             )
 
-        def project(n):
-            product[n] = psum_a.tile([P, HALVES, BANK], F32, name="product", tag="product")
+        def project(t):
+            product[t] = psum_a.tile([P, HALVES, BANK], F32, name="product", tag="product")
             for h in range(HALVES):
                 for g in range(PASSES):
                     nc.tensor.matmul_mx(
-                        out=product[n][:, h, :],
-                        lhsT=codes[n][:, P * g : P * (g + 1)].bitcast(FP8X4),
-                        lhsT_scale=planes[n][:, P * g : P * (g + 1)],
+                        out=product[t][:, h, :],
+                        lhsT=codes[t][:, P * g : P * (g + 1)].bitcast(FP8X4),
+                        lhsT_scale=planes[t][:, P * g : P * (g + 1)],
                         rhs=w_words[:, g, 2 * BANK * h : 2 * BANK * (h + 1)].bitcast(FP4X4),
                         rhs_scale=w_planes[:, g, BANK * h : BANK * (h + 1)],
                         start=(g == 0),
                         stop=(g == PASSES - 1),
                     )
 
-        def add_bias(n):
-            biased[n] = per_tile.tile([P, C], F32, name="biased", tag="biased")
-            sums[n] = per_tile.tile([P, HALVES], F32, name="sums", tag="sums")
+        def add_bias(t):
+            biased[t] = per_tile.tile([P, C], F32, name="biased", tag="biased")
             for h in range(HALVES):
                 nc.vector.scalar_tensor_tensor(
-                    out=biased[n][:, BANK * h : BANK * (h + 1)],
-                    in0=product[n][:, h, :],
+                    out=biased[t][:, BANK * h : BANK * (h + 1)],
+                    in0=product[t][:, h, :],
                     scalar=1.0,
                     in1=bias_all[:, BANK * h : BANK * (h + 1)],
                     op0=ALU.mult,
                     op1=ALU.add,
-                    accum_out=sums[n][:, h : h + 1],
+                    accum_out=sums[:, t, h : h + 1],
                 )
 
-        def mean(n):
-            neg_mean[n] = per_tile.tile([P, 1], F32, name="neg_mean", tag="neg_mean")
-            nc.gpsimd.tensor_scalar(
-                out=neg_mean[n][:],
-                in0=sums[n][:, 0:1],
-                scalar1=sums[n][:, 1:2],
+        def mean(t):
+            nc.vector.tensor_scalar(
+                out=neg_mean[:, t : t + 1],
+                in0=sums[:, t, 0:1],
+                scalar1=sums[:, t, 1:2],
                 scalar2=-1.0 / C,
                 op0=ALU.add,
                 op1=ALU.mult,
             )
 
-        def square(n):
+        def square(t):
             squares = per_tile.tile([P, C], BF16, name="squares", tag="squares")
-            sum_squares[n] = per_tile.tile([P, 1], F32, name="sum_squares", tag="sum_squares")
             nc.scalar.activation(
-                out=squares[:], in_=biased[n][:], func=ACT.Square, bias=neg_mean[n][:], accum_out=sum_squares[n][:]
+                out=squares[:],
+                in_=biased[t][:],
+                func=ACT.Square,
+                bias=neg_mean[:, t : t + 1],
+                accum_out=sum_squares[:, t : t + 1],
             )
 
-        def root(n):
-            deviation[n] = per_tile.tile([P, 1], F32, name="deviation", tag="deviation")
-            nc.scalar.activation(out=deviation[n][:], in_=sum_squares[n][:], func=ACT.Sqrt, scale=1.0 / (C - 1))
-
-        def fold(n):
-            t = first_token(n) // P
-            padded = per_tile.tile([P, 1], F32, name="padded", tag="padded")
-            inverse = per_tile.tile([P, 1], F32, name="inverse", tag="inverse")
-            gain[n] = per_tile.tile([P, 1], F32, name="gain", tag="gain")
-            offset[n] = per_tile.tile([P, 1], F32, name="offset", tag="offset")
+        def fold(first):
+            tiles = slice(first, first + GROUP)
+            shifts = slice(N_TILES + first, N_TILES + first + GROUP)
+            nc.gpsimd.tensor_tensor(out=root[:, tiles], in0=sum_squares[:, tiles], in1=one_half[:], op=ALU.pow)
             nc.gpsimd.tensor_scalar(
-                out=padded[:], in0=deviation[n][:], scalar1=1.0, scalar2=EPS, op0=ALU.mult, op1=ALU.add
+                out=padded[:, tiles], in0=root[:, tiles], scalar1=(C - 1) ** -0.5, scalar2=EPS, op0=ALU.mult, op1=ALU.add
             )
-            nc.gpsimd.tensor_tensor(out=inverse[:], in0=padded[:], in1=minus_one[:], op=ALU.pow)
-            nc.gpsimd.tensor_tensor(out=gain[n][:], in0=inverse[:], in1=token_columns[:, t : t + 1], op=ALU.mult)
-            nc.gpsimd.tensor_scalar(
-                out=offset[n][:],
-                in0=neg_mean[n][:],
-                scalar1=gain[n][:],
-                scalar2=token_columns[:, N_TILES + t : N_TILES + t + 1],
-                op0=ALU.mult,
-                op1=ALU.add,
-            )
+            nc.gpsimd.tensor_tensor(out=inverse[:, tiles], in0=padded[:, tiles], in1=minus_one[:], op=ALU.pow)
+            nc.gpsimd.tensor_tensor(out=gain[:, tiles], in0=inverse[:, tiles], in1=token_columns[:, tiles], op=ALU.mult)
+            nc.gpsimd.tensor_tensor(out=mean_gain[:, tiles], in0=neg_mean[:, tiles], in1=gain[:, tiles], op=ALU.mult)
+            nc.gpsimd.tensor_tensor(out=offset[:, tiles], in0=mean_gain[:, tiles], in1=token_columns[:, shifts], op=ALU.add)
 
-        def normalise(n):
-            result[n] = per_tile.tile([P, C], F32, name="result", tag="result")
-            nc.scalar.activation(
-                out=result[n][:], in_=biased[n][:], func=ACT.Identity, scale=gain[n][:], bias=offset[n][:]
-            )
+        def normalise(t):
+            result[t] = per_tile.tile([P, C], F32, name="result", tag="result")
+            if t < VECTOR_TILES:
+                nc.vector.tensor_scalar(
+                    out=result[t][:],
+                    in0=biased[t][:],
+                    scalar1=gain[:, t : t + 1],
+                    scalar2=offset[:, t : t + 1],
+                    op0=ALU.mult,
+                    op1=ALU.add,
+                )
+            else:
+                nc.scalar.activation(
+                    out=result[t][:],
+                    in_=biased[t][:],
+                    func=ACT.Identity,
+                    scale=gain[:, t : t + 1],
+                    bias=offset[:, t : t + 1],
+                )
 
-        def add_residual_and_store(n):
-            nc.vector.tensor_add(out=result[n][:], in0=result[n][:], in1=residual[:, first_token(n) // P, :])
-            nc.sync.dma_start(out=out[0, first_token(n) : first_token(n) + P, :], in_=result[n][:])
+        def add_residual_and_store(t):
+            nc.vector.tensor_add(out=result[t][:], in0=result[t][:], in1=residual[:, t, :])
+            nc.sync.dma_start(out=out[0, P * t : P * (t + 1), :], in_=result[t][:])
 
         bias_bank = psum_a.tile([P, HALVES, BANK], F32, name="bias_bank", tag="product")
         bias_all = keep.tile([P, C], F32, name="bias_all")
@@ -244,6 +249,11 @@ def tile_swintransformerblock_pb_kernel(
         transpose(2)
         quantise(1)
         project(1)
+        copy_out(2)
+        transpose(3)
+
+        def live(t):
+            return 0 <= t < N_TILES
 
         token_rows_f32 = keep.tile([P, P], F32, name="token_rows_f32")
         token_columns = keep.tile([P, 2 * N_TILES], F32, name="token_columns")
@@ -252,30 +262,29 @@ def tile_swintransformerblock_pb_kernel(
             token_bank = psum_t.tile([P, P], F32, name="token_bank", tag="transposed")
             nc.gpsimd.tensor_copy(out=token_rows_f32[:], in_=token_rows[:])
             nc.tensor.transpose(token_bank[:], token_rows_f32[:], identity[:])
-            nc.scalar.copy(out=token_columns[:], in_=token_bank[:, 0 : 2 * N_TILES])
+            nc.vector.tensor_copy(out=token_columns[:], in_=token_bank[:, 0 : 2 * N_TILES])
 
-        def live(n):
-            return 0 <= n < N_TILES
+        after_last_product = N_TILES - 2
 
-        for step in range(N_TILES + 4):
-            if live(step - 1):
-                square(step - 1)
-            if live(step + 3):
-                transpose(step + 3)
-            if live(step):
-                add_bias(step)
-                mean(step)
-            if live(step + 2):
-                copy_out(step + 2)
-            if live(step - 1):
-                root(step - 1)
-                fold(step - 1)
-            if live(step - 3):
-                add_residual_and_store(step - 3)
-            if live(step + 2):
-                quantise(step + 2)
-                project(step + 2)
-            if step == 0:
+        for t in range(N_TILES + 1):
+            if live(t - 1):
+                square(t - 1)
+            if live(t + 4):
+                transpose(t + 4)
+            if live(t):
+                add_bias(t)
+            if live(t + 3):
+                copy_out(t + 3)
+            if live(t + 2):
+                quantise(t + 2)
+                project(t + 2)
+            if t == after_last_product:
                 spread_token_vectors()
-            if live(step - 2):
-                normalise(step - 2)
+                fold(0)
+            if live(t):
+                mean(t)
+        fold(GROUP)
+
+        for t in range(N_TILES):
+            normalise(t)
+            add_residual_and_store(t)

@@ -29,7 +29,7 @@ SHIFT = 4
 ROWS_IN_TILE = P // GRID
 EPS = 1e-5
 GROUP = N_TILES // 2
-VECTOR_TILES = 2
+VECTOR_TILES = 1
 
 FLOPS = 2 * TOKENS * C * C
 
@@ -49,21 +49,17 @@ def tile_swintransformerblock_pb_kernel(
         w_planes = keep.tile([P, PASSES, C], U8, name="w_planes", align_bytes=64)
         token_rows = keep.tile([P, P], BF16, name="token_rows")
         ones = keep.tile([P, P], BF16, name="ones")
-        one_half = keep.tile([P, GROUP], F32, name="one_half")
-        minus_one = keep.tile([P, GROUP], F32, name="minus_one")
         nc.vector.memset(bias_rows[:], 0.0)
         nc.vector.memset(w_planes[:].rearrange("p g n -> p (g n)").bitcast(I32), 0)
         nc.vector.memset(token_rows[:], 0.0)
         nc.vector.memset(ones[:], 1.0)
-        nc.vector.memset(one_half[:], 0.5)
-        nc.vector.memset(minus_one[:], -1.0)
 
         identity = keep.tile([P, P], F32, name="identity")
         make_identity(nc, identity[:])
 
         nc.scalar.dma_start(out=bias_rows[0:1, :], in_=out_b.rearrange("(o c) -> o c", o=1))
         table_warmer = keep.tile([P, 1], F32, name="table_warmer")
-        nc.scalar.activation(out=table_warmer[:], in_=ones[:, 0:1], func=ACT.Square)
+        nc.scalar.activation(out=table_warmer[:], in_=ones[:, 0:1], func=ACT.Sqrt)
 
         attention = [per_tile.tile([P, C], BF16, name="attention", tag="attention") for t in range(N_TILES)]
         residual = keep.tile([P, N_TILES, C], BF16, name="residual")
@@ -118,7 +114,7 @@ def tile_swintransformerblock_pb_kernel(
         sums = keep.tile([P, N_TILES, HALVES], F32, name="sums")
         neg_mean = keep.tile([P, N_TILES], F32, name="neg_mean")
         sum_squares = keep.tile([P, N_TILES], F32, name="sum_squares")
-        root = keep.tile([P, N_TILES], F32, name="root")
+        deviation = keep.tile([P, N_TILES], F32, name="deviation")
         padded = keep.tile([P, N_TILES], F32, name="padded")
         inverse = keep.tile([P, N_TILES], F32, name="inverse")
         gain = keep.tile([P, N_TILES], F32, name="gain")
@@ -199,14 +195,12 @@ def tile_swintransformerblock_pb_kernel(
         def fold(first):
             tiles = slice(first, first + GROUP)
             shifts = slice(N_TILES + first, N_TILES + first + GROUP)
-            nc.gpsimd.tensor_tensor(out=root[:, tiles], in0=sum_squares[:, tiles], in1=one_half[:], op=ALU.pow)
-            nc.gpsimd.tensor_scalar(
-                out=padded[:, tiles], in0=root[:, tiles], scalar1=(C - 1) ** -0.5, scalar2=EPS, op0=ALU.mult, op1=ALU.add
-            )
-            nc.gpsimd.tensor_tensor(out=inverse[:, tiles], in0=padded[:, tiles], in1=minus_one[:], op=ALU.pow)
-            nc.gpsimd.tensor_tensor(out=gain[:, tiles], in0=inverse[:, tiles], in1=token_columns[:, tiles], op=ALU.mult)
-            nc.gpsimd.tensor_tensor(out=mean_gain[:, tiles], in0=neg_mean[:, tiles], in1=gain[:, tiles], op=ALU.mult)
-            nc.gpsimd.tensor_tensor(out=offset[:, tiles], in0=mean_gain[:, tiles], in1=token_columns[:, shifts], op=ALU.add)
+            nc.scalar.activation(out=deviation[:, tiles], in_=sum_squares[:, tiles], func=ACT.Sqrt, scale=1.0 / (C - 1))
+            nc.vector.tensor_scalar_add(out=padded[:, tiles], in0=deviation[:, tiles], scalar1=EPS)
+            nc.vector.reciprocal(out=inverse[:, tiles], in_=padded[:, tiles])
+            nc.vector.tensor_mul(out=gain[:, tiles], in0=inverse[:, tiles], in1=token_columns[:, tiles])
+            nc.vector.tensor_mul(out=mean_gain[:, tiles], in0=neg_mean[:, tiles], in1=gain[:, tiles])
+            nc.vector.tensor_add(out=offset[:, tiles], in0=mean_gain[:, tiles], in1=token_columns[:, shifts])
 
         def normalise(t):
             result[t] = per_tile.tile([P, C], F32, name="result", tag="result")
@@ -283,8 +277,9 @@ def tile_swintransformerblock_pb_kernel(
                 fold(0)
             if live(t):
                 mean(t)
-        fold(GROUP)
 
         for t in range(N_TILES):
+            if t == VECTOR_TILES:
+                fold(GROUP)
             normalise(t)
             add_residual_and_store(t)

@@ -29,7 +29,7 @@ SHIFT = 4
 ROWS_IN_TILE = P // GRID
 EPS = 1e-5
 GROUP = N_TILES // 2
-VECTOR_TILES = 1
+VECTOR_TILES = 2
 
 FLOPS = 2 * TOKENS * C * C
 
@@ -49,10 +49,12 @@ def tile_swintransformerblock_pb_kernel(
         w_planes = keep.tile([P, PASSES, C], U8, name="w_planes", align_bytes=64)
         token_rows = keep.tile([P, P], BF16, name="token_rows")
         ones = keep.tile([P, P], BF16, name="ones")
+        minus_one = keep.tile([P, GROUP], F32, name="minus_one")
         nc.vector.memset(bias_rows[:], 0.0)
         nc.vector.memset(w_planes[:].rearrange("p g n -> p (g n)").bitcast(I32), 0)
         nc.vector.memset(token_rows[:], 0.0)
         nc.vector.memset(ones[:], 1.0)
+        nc.vector.memset(minus_one[:], -1.0)
 
         identity = keep.tile([P, P], F32, name="identity")
         make_identity(nc, identity[:])
@@ -74,7 +76,8 @@ def tile_swintransformerblock_pb_kernel(
                 ].rearrange("w q c -> q w c"),
             )
 
-        load_attention(0)
+        for t in range(N_TILES):
+            load_attention(t)
         w_words = keep.tile([P, PASSES, 2 * C], U8, name="w_words", align_bytes=64)
         nc.sync.dma_start(out=w_words[:].bitcast(I32), in_=out_w_words.rearrange("g p b -> p g b").bitcast(I32))
         for quadrant in range(4):
@@ -82,8 +85,6 @@ def tile_swintransformerblock_pb_kernel(
                 out=w_planes[32 * quadrant : 32 * quadrant + 4, :, :].bitcast(I32),
                 in_=out_w_scales[:, 4 * quadrant : 4 * quadrant + 4, :].rearrange("g r n -> r g n").bitcast(I32),
             )
-        for t in range(1, N_TILES):
-            load_attention(t)
         nc.sync.dma_start(out=token_rows[0:N_TILES, :], in_=ada1_scale.rearrange("o (t p) i -> (o t) (p i)", p=P))
         nc.sync.dma_start(
             out=token_rows[N_TILES : 2 * N_TILES, :], in_=ada1_shift.rearrange("o (t p) i -> (o t) (p i)", p=P)
@@ -109,17 +110,18 @@ def tile_swintransformerblock_pb_kernel(
         codes = {}
         planes = {}
         product = {}
-        biased = {}
+        biased = [per_tile.tile([P, C], F32, name="biased", tag="biased") for t in range(N_TILES)]
         result = {}
         sums = keep.tile([P, N_TILES, HALVES], F32, name="sums")
         neg_mean = keep.tile([P, N_TILES], F32, name="neg_mean")
         sum_squares = keep.tile([P, N_TILES], F32, name="sum_squares")
         deviation = keep.tile([P, N_TILES], F32, name="deviation")
         padded = keep.tile([P, N_TILES], F32, name="padded")
-        inverse = keep.tile([P, N_TILES], F32, name="inverse")
-        gain = keep.tile([P, N_TILES], F32, name="gain")
-        mean_gain = keep.tile([P, N_TILES], F32, name="mean_gain")
-        offset = keep.tile([P, N_TILES], F32, name="offset")
+        groups = range(0, N_TILES, GROUP)
+        inverse = {first: keep.tile([P, GROUP], F32, name="inverse%d" % first) for first in groups}
+        gain = {first: keep.tile([P, GROUP], F32, name="gain%d" % first) for first in groups}
+        mean_gain = {first: keep.tile([P, GROUP], F32, name="mean_gain%d" % first) for first in groups}
+        offset = {first: keep.tile([P, GROUP], F32, name="offset%d" % first) for first in groups}
 
         def transpose(t):
             transposed[t] = psum_t.tile([P, PASSES, 2, P], F32, name="transposed", tag="transposed")
@@ -159,18 +161,16 @@ def tile_swintransformerblock_pb_kernel(
                         stop=(g == PASSES - 1),
                     )
 
-        def add_bias(t):
-            biased[t] = per_tile.tile([P, C], F32, name="biased", tag="biased")
-            for h in range(HALVES):
-                nc.vector.scalar_tensor_tensor(
-                    out=biased[t][:, BANK * h : BANK * (h + 1)],
-                    in0=product[t][:, h, :],
-                    scalar=1.0,
-                    in1=bias_all[:, BANK * h : BANK * (h + 1)],
-                    op0=ALU.mult,
-                    op1=ALU.add,
-                    accum_out=sums[:, t, h : h + 1],
-                )
+        def add_bias(t, h):
+            nc.vector.scalar_tensor_tensor(
+                out=biased[t][:, BANK * h : BANK * (h + 1)],
+                in0=product[t][:, h, :],
+                scalar=1.0,
+                in1=bias_all[:, BANK * h : BANK * (h + 1)],
+                op0=ALU.mult,
+                op1=ALU.add,
+                accum_out=sums[:, t, h : h + 1],
+            )
 
         def mean(t):
             nc.vector.tensor_scalar(
@@ -192,94 +192,76 @@ def tile_swintransformerblock_pb_kernel(
                 accum_out=sum_squares[:, t : t + 1],
             )
 
-        def fold(first):
+        def root(first):
+            tiles = slice(first, first + GROUP)
+            nc.scalar.activation(out=deviation[:, tiles], in_=sum_squares[:, tiles], func=ACT.Sqrt, scale=1.0 / (C - 1))
+            nc.scalar.activation(out=padded[:, tiles], in_=deviation[:, tiles], func=ACT.Identity, bias=EPS)
+
+        def fold(first, engine):
             tiles = slice(first, first + GROUP)
             shifts = slice(N_TILES + first, N_TILES + first + GROUP)
-            nc.scalar.activation(out=deviation[:, tiles], in_=sum_squares[:, tiles], func=ACT.Sqrt, scale=1.0 / (C - 1))
-            nc.vector.tensor_scalar_add(out=padded[:, tiles], in0=deviation[:, tiles], scalar1=EPS)
-            nc.vector.reciprocal(out=inverse[:, tiles], in_=padded[:, tiles])
-            nc.vector.tensor_mul(out=gain[:, tiles], in0=inverse[:, tiles], in1=token_columns[:, tiles])
-            nc.vector.tensor_mul(out=mean_gain[:, tiles], in0=neg_mean[:, tiles], in1=gain[:, tiles])
-            nc.vector.tensor_add(out=offset[:, tiles], in0=mean_gain[:, tiles], in1=token_columns[:, shifts])
+            engine.tensor_tensor(out=gain[first][:], in0=inverse[first][:], in1=token_columns[:, tiles], op=ALU.mult)
+            engine.tensor_tensor(out=mean_gain[first][:], in0=neg_mean[:, tiles], in1=gain[first][:], op=ALU.mult)
+            engine.tensor_tensor(out=offset[first][:], in0=mean_gain[first][:], in1=token_columns[:, shifts], op=ALU.add)
 
         def normalise(t):
             result[t] = per_tile.tile([P, C], F32, name="result", tag="result")
+            first, column = t - t % GROUP, t % GROUP
+            tile_gain = gain[first][:, column : column + 1]
+            tile_offset = offset[first][:, column : column + 1]
             if t < VECTOR_TILES:
                 nc.vector.tensor_scalar(
-                    out=result[t][:],
-                    in0=biased[t][:],
-                    scalar1=gain[:, t : t + 1],
-                    scalar2=offset[:, t : t + 1],
-                    op0=ALU.mult,
-                    op1=ALU.add,
+                    out=result[t][:], in0=biased[t][:], scalar1=tile_gain, scalar2=tile_offset, op0=ALU.mult, op1=ALU.add
                 )
             else:
                 nc.scalar.activation(
-                    out=result[t][:],
-                    in_=biased[t][:],
-                    func=ACT.Identity,
-                    scale=gain[:, t : t + 1],
-                    bias=offset[:, t : t + 1],
+                    out=result[t][:], in_=biased[t][:], func=ACT.Identity, scale=tile_gain, bias=tile_offset
                 )
 
         def add_residual_and_store(t):
             nc.vector.tensor_add(out=result[t][:], in0=result[t][:], in1=residual[:, t, :])
             nc.sync.dma_start(out=out[0, P * t : P * (t + 1), :], in_=result[t][:])
 
+        for t in range(N_TILES):
+            transpose(t)
+            copy_out(t)
+            quantise(t)
+
         bias_bank = psum_a.tile([P, HALVES, BANK], F32, name="bias_bank", tag="product")
         bias_all = keep.tile([P, C], F32, name="bias_all")
-        transpose(0)
-        copy_out(0)
-        transpose(1)
         for h in range(HALVES):
             nc.tensor.matmul(
                 out=bias_bank[:, h, :], lhsT=ones[:], rhs=bias_rows[:, BANK * h : BANK * (h + 1)], start=True, stop=True
             )
-        quantise(0)
-        project(0)
-        copy_out(1)
         nc.vector.tensor_copy(out=bias_all[:, 0:BANK], in_=bias_bank[:, 0, :])
         nc.scalar.copy(out=bias_all[:, BANK:C], in_=bias_bank[:, 1, :])
-        transpose(2)
-        quantise(1)
-        project(1)
-        copy_out(2)
-        transpose(3)
-
-        def live(t):
-            return 0 <= t < N_TILES
 
         token_rows_f32 = keep.tile([P, P], F32, name="token_rows_f32")
+        token_bank = psum_t.tile([P, P], F32, name="token_bank", tag="transposed")
         token_columns = keep.tile([P, 2 * N_TILES], F32, name="token_columns")
+        nc.gpsimd.tensor_copy(out=token_rows_f32[:], in_=token_rows[:])
 
-        def spread_token_vectors():
-            token_bank = psum_t.tile([P, P], F32, name="token_bank", tag="transposed")
-            nc.gpsimd.tensor_copy(out=token_rows_f32[:], in_=token_rows[:])
-            nc.tensor.transpose(token_bank[:], token_rows_f32[:], identity[:])
-            nc.vector.tensor_copy(out=token_columns[:], in_=token_bank[:, 0 : 2 * N_TILES])
-
-        after_last_product = N_TILES - 2
-
-        for t in range(N_TILES + 1):
-            if live(t - 1):
+        for t in range(N_TILES):
+            project(t)
+            add_bias(t, 0)
+            if t > 0:
+                mean(t - 1)
                 square(t - 1)
-            if live(t + 4):
-                transpose(t + 4)
-            if live(t):
-                add_bias(t)
-            if live(t + 3):
-                copy_out(t + 3)
-            if live(t + 2):
-                quantise(t + 2)
-                project(t + 2)
-            if t == after_last_product:
-                spread_token_vectors()
-                fold(0)
-            if live(t):
-                mean(t)
+            add_bias(t, 1)
+            if t == GROUP - 1:
+                nc.tensor.transpose(token_bank[:], token_rows_f32[:], identity[:])
+                nc.scalar.copy(out=token_columns[:], in_=token_bank[:, 0 : 2 * N_TILES])
+            if t == GROUP:
+                root(0)
+                nc.gpsimd.tensor_tensor(out=inverse[0][:], in0=padded[:, 0:GROUP], in1=minus_one[:], op=ALU.pow)
+                fold(0, nc.gpsimd)
+        mean(N_TILES - 1)
+        square(N_TILES - 1)
+        root(GROUP)
 
         for t in range(N_TILES):
             if t == VECTOR_TILES:
-                fold(GROUP)
+                nc.vector.reciprocal(out=inverse[GROUP][:], in_=padded[:, GROUP:N_TILES])
+                fold(GROUP, nc.vector)
             normalise(t)
             add_residual_and_store(t)

@@ -29,6 +29,7 @@ SHIFT = 4
 ROWS_IN_TILE = P // GRID
 EPS = 1e-5
 GROUP = N_TILES // 2
+LAST_PIECES = 2
 VECTOR_TILES = 2
 
 FLOPS = 2 * TOKENS * C * C
@@ -41,8 +42,8 @@ def tile_swintransformerblock_pb_kernel(
     with ExitStack() as ctx:
         keep = ctx.enter_context(tc.tile_pool(name="keep", bufs=1))
         per_tile = ctx.enter_context(tc.tile_pool(name="per_tile", bufs=N_TILES))
-        psum_t = ctx.enter_context(tc.psum_pool(name="psum_t", bufs=2))
-        psum_a = ctx.enter_context(tc.psum_pool(name="psum_a", bufs=3))
+        psum_t = ctx.enter_context(tc.psum_pool(name="psum_t", bufs=4))
+        psum_a = ctx.enter_context(tc.psum_pool(name="psum_a", bufs=4))
         ctx.enter_context(tc.manual_schedule())
 
         bias_rows = keep.tile([P, C], BF16, name="bias_rows")
@@ -148,11 +149,11 @@ def tile_swintransformerblock_pb_kernel(
             )
 
         def project(t):
-            product[t] = psum_a.tile([P, HALVES, BANK], F32, name="product", tag="product")
             for h in range(HALVES):
+                product[t, h] = psum_a.tile([P, BANK], F32, name="product", tag="product")
                 for g in range(PASSES):
                     nc.tensor.matmul_mx(
-                        out=product[t][:, h, :],
+                        out=product[t, h][:],
                         lhsT=codes[t][:, P * g : P * (g + 1)].bitcast(FP8X4),
                         lhsT_scale=planes[t][:, P * g : P * (g + 1)],
                         rhs=w_words[:, g, 2 * BANK * h : 2 * BANK * (h + 1)].bitcast(FP4X4),
@@ -164,7 +165,7 @@ def tile_swintransformerblock_pb_kernel(
         def add_bias(t, h):
             nc.vector.scalar_tensor_tensor(
                 out=biased[t][:, BANK * h : BANK * (h + 1)],
-                in0=product[t][:, h, :],
+                in0=product[t, h][:],
                 scalar=1.0,
                 in1=bias_all[:, BANK * h : BANK * (h + 1)],
                 op0=ALU.mult,
@@ -219,22 +220,26 @@ def tile_swintransformerblock_pb_kernel(
                 )
 
         def add_residual_and_store(t):
-            nc.vector.tensor_add(out=result[t][:], in0=result[t][:], in1=residual[:, t, :])
-            nc.sync.dma_start(out=out[0, P * t : P * (t + 1), :], in_=result[t][:])
+            width = C // (LAST_PIECES if t == N_TILES - 1 else 1)
+            for c in range(0, C, width):
+                nc.vector.tensor_add(
+                    out=result[t][:, c : c + width], in0=result[t][:, c : c + width], in1=residual[:, t, c : c + width]
+                )
+                nc.sync.dma_start(out=out[0, P * t : P * (t + 1), c : c + width], in_=result[t][:, c : c + width])
 
         for t in range(N_TILES):
             transpose(t)
             copy_out(t)
             quantise(t)
 
-        bias_bank = psum_a.tile([P, HALVES, BANK], F32, name="bias_bank", tag="product")
+        bias_bank = [psum_a.tile([P, BANK], F32, name="bias_bank", tag="product") for h in range(HALVES)]
         bias_all = keep.tile([P, C], F32, name="bias_all")
         for h in range(HALVES):
             nc.tensor.matmul(
-                out=bias_bank[:, h, :], lhsT=ones[:], rhs=bias_rows[:, BANK * h : BANK * (h + 1)], start=True, stop=True
+                out=bias_bank[h][:], lhsT=ones[:], rhs=bias_rows[:, BANK * h : BANK * (h + 1)], start=True, stop=True
             )
-        nc.vector.tensor_copy(out=bias_all[:, 0:BANK], in_=bias_bank[:, 0, :])
-        nc.scalar.copy(out=bias_all[:, BANK:C], in_=bias_bank[:, 1, :])
+        nc.vector.tensor_copy(out=bias_all[:, 0:BANK], in_=bias_bank[0][:])
+        nc.scalar.copy(out=bias_all[:, BANK:C], in_=bias_bank[1][:])
 
         token_rows_f32 = keep.tile([P, P], F32, name="token_rows_f32")
         token_bank = psum_t.tile([P, P], F32, name="token_bank", tag="transposed")

@@ -227,10 +227,13 @@ def tile_swintransformerblock_pb_kernel(
                 )
                 nc.sync.dma_start(out=out[0, P * t : P * (t + 1), c : c + width], in_=result[t][:, c : c + width])
 
-        for t in range(N_TILES):
+        def prepare(t):
             transpose(t)
             copy_out(t)
             quantise(t)
+
+        for t in range(GROUP):
+            prepare(t)
 
         bias_bank = [psum_a.tile([P, BANK], F32, name="bias_bank", tag="product") for h in range(HALVES)]
         bias_all = keep.tile([P, C], F32, name="bias_all")
@@ -240,6 +243,9 @@ def tile_swintransformerblock_pb_kernel(
             )
         nc.vector.tensor_copy(out=bias_all[:, 0:BANK], in_=bias_bank[0][:])
         nc.scalar.copy(out=bias_all[:, BANK:C], in_=bias_bank[1][:])
+
+        for t in range(GROUP, N_TILES):
+            prepare(t)
 
         token_rows_f32 = keep.tile([P, P], F32, name="token_rows_f32")
         token_bank = psum_t.tile([P, P], F32, name="token_bank", tag="transposed")

@@ -28,9 +28,10 @@ GRID = 32
 SHIFT = 4
 ROWS_IN_TILE = P // GRID
 EPS = 1e-5
-GROUP = N_TILES // 2
+HALF = N_TILES // 2
+GROUP = 2
 LAST_PIECES = 2
-VECTOR_TILES = 2
+GPSIMD_TILES = 3
 
 FLOPS = 2 * TOKENS * C * C
 
@@ -50,17 +51,19 @@ def tile_swintransformerblock_pb_kernel(
         w_planes = keep.tile([P, PASSES, C], U8, name="w_planes", align_bytes=64)
         token_rows = keep.tile([P, P], BF16, name="token_rows")
         ones = keep.tile([P, P], BF16, name="ones")
-        minus_one = keep.tile([P, GROUP], F32, name="minus_one")
         nc.vector.memset(bias_rows[:], 0.0)
         nc.vector.memset(w_planes[:].rearrange("p g n -> p (g n)").bitcast(I32), 0)
         nc.vector.memset(token_rows[:], 0.0)
         nc.vector.memset(ones[:], 1.0)
-        nc.vector.memset(minus_one[:], -1.0)
 
         identity = keep.tile([P, P], F32, name="identity")
         make_identity(nc, identity[:])
 
         nc.scalar.dma_start(out=bias_rows[0:1, :], in_=out_b.rearrange("(o c) -> o c", o=1))
+        nc.scalar.dma_start(out=token_rows[0:N_TILES, :], in_=ada1_scale.rearrange("o (t p) i -> (o t) (p i)", p=P))
+        nc.scalar.dma_start(
+            out=token_rows[N_TILES : 2 * N_TILES, :], in_=ada1_shift.rearrange("o (t p) i -> (o t) (p i)", p=P)
+        )
         table_warmer = keep.tile([P, 1], F32, name="table_warmer")
         nc.scalar.activation(out=table_warmer[:], in_=ones[:, 0:1], func=ACT.Sqrt)
 
@@ -86,10 +89,6 @@ def tile_swintransformerblock_pb_kernel(
                 out=w_planes[32 * quadrant : 32 * quadrant + 4, :, :].bitcast(I32),
                 in_=out_w_scales[:, 4 * quadrant : 4 * quadrant + 4, :].rearrange("g r n -> r g n").bitcast(I32),
             )
-        nc.sync.dma_start(out=token_rows[0:N_TILES, :], in_=ada1_scale.rearrange("o (t p) i -> (o t) (p i)", p=P))
-        nc.sync.dma_start(
-            out=token_rows[N_TILES : 2 * N_TILES, :], in_=ada1_shift.rearrange("o (t p) i -> (o t) (p i)", p=P)
-        )
         for t in range(0, N_TILES, 2):
             nc.sync.dma_start(
                 out=residual[:, t : t + 2, :], in_=x[0, P * t : P * (t + 2), :].rearrange("(t p) c -> p t c", p=P)
@@ -117,12 +116,9 @@ def tile_swintransformerblock_pb_kernel(
         neg_mean = keep.tile([P, N_TILES], F32, name="neg_mean")
         sum_squares = keep.tile([P, N_TILES], F32, name="sum_squares")
         deviation = keep.tile([P, N_TILES], F32, name="deviation")
-        padded = keep.tile([P, N_TILES], F32, name="padded")
-        groups = range(0, N_TILES, GROUP)
-        inverse = {first: keep.tile([P, GROUP], F32, name="inverse%d" % first) for first in groups}
-        gain = {first: keep.tile([P, GROUP], F32, name="gain%d" % first) for first in groups}
-        mean_gain = {first: keep.tile([P, GROUP], F32, name="mean_gain%d" % first) for first in groups}
-        offset = {first: keep.tile([P, GROUP], F32, name="offset%d" % first) for first in groups}
+        divisor = keep.tile([P, N_TILES], F32, name="divisor")
+        gain = keep.tile([P, N_TILES], F32, name="gain")
+        mean_gain = keep.tile([P, N_TILES], F32, name="mean_gain")
 
         def transpose(t):
             transposed[t] = psum_t.tile([P, PASSES, 2, P], F32, name="transposed", tag="transposed")
@@ -196,34 +192,59 @@ def tile_swintransformerblock_pb_kernel(
         def root(first):
             tiles = slice(first, first + GROUP)
             nc.scalar.activation(out=deviation[:, tiles], in_=sum_squares[:, tiles], func=ACT.Sqrt, scale=1.0 / (C - 1))
-            nc.scalar.activation(out=padded[:, tiles], in_=deviation[:, tiles], func=ACT.Identity, bias=EPS)
 
-        def fold(first, engine):
+        def divide(first):
             tiles = slice(first, first + GROUP)
-            shifts = slice(N_TILES + first, N_TILES + first + GROUP)
-            engine.tensor_tensor(out=gain[first][:], in0=inverse[first][:], in1=token_columns[:, tiles], op=ALU.mult)
-            engine.tensor_tensor(out=mean_gain[first][:], in0=neg_mean[:, tiles], in1=gain[first][:], op=ALU.mult)
-            engine.tensor_tensor(out=offset[first][:], in0=mean_gain[first][:], in1=token_columns[:, shifts], op=ALU.add)
+            nc.vector.scalar_tensor_tensor(
+                out=divisor[:, tiles],
+                in0=deviation[:, tiles],
+                scalar=EPS,
+                in1=inverse_scale[:, tiles],
+                op0=ALU.add,
+                op1=ALU.mult,
+            )
+
+        def invert(first):
+            tiles = slice(first, first + GROUP)
+            nc.vector.reciprocal(out=gain[:, tiles], in_=divisor[:, tiles])
+
+        def fold(first):
+            tiles = slice(max(first, GPSIMD_TILES), first + GROUP)
+            if tiles.start < tiles.stop:
+                nc.vector.tensor_tensor(
+                    out=mean_gain[:, tiles], in0=neg_mean[:, tiles], in1=gain[:, tiles], op=ALU.mult
+                )
 
         def normalise(t):
             result[t] = per_tile.tile([P, C], F32, name="result", tag="result")
-            first, column = t - t % GROUP, t % GROUP
-            tile_gain = gain[first][:, column : column + 1]
-            tile_offset = offset[first][:, column : column + 1]
-            if t < VECTOR_TILES:
-                nc.vector.tensor_scalar(
-                    out=result[t][:], in0=biased[t][:], scalar1=tile_gain, scalar2=tile_offset, op0=ALU.mult, op1=ALU.add
+            if t < GPSIMD_TILES:
+                nc.gpsimd.tensor_scalar(
+                    out=result[t][:],
+                    in0=biased[t][:],
+                    scalar1=neg_mean[:, t : t + 1],
+                    scalar2=gain[:, t : t + 1],
+                    op0=ALU.add,
+                    op1=ALU.mult,
                 )
             else:
                 nc.scalar.activation(
-                    out=result[t][:], in_=biased[t][:], func=ACT.Identity, scale=tile_gain, bias=tile_offset
+                    out=result[t][:],
+                    in_=biased[t][:],
+                    func=ACT.Identity,
+                    scale=gain[:, t : t + 1],
+                    bias=mean_gain[:, t : t + 1],
                 )
 
         def add_residual_and_store(t):
             width = C // (LAST_PIECES if t == N_TILES - 1 else 1)
             for c in range(0, C, width):
-                nc.vector.tensor_add(
-                    out=result[t][:, c : c + width], in0=result[t][:, c : c + width], in1=residual[:, t, c : c + width]
+                nc.vector.scalar_tensor_tensor(
+                    out=result[t][:, c : c + width],
+                    in0=result[t][:, c : c + width],
+                    scalar=token_columns[:, N_TILES + t : N_TILES + t + 1],
+                    in1=residual[:, t, c : c + width],
+                    op0=ALU.add,
+                    op1=ALU.add,
                 )
                 nc.sync.dma_start(out=out[0, P * t : P * (t + 1), c : c + width], in_=result[t][:, c : c + width])
 
@@ -232,7 +253,7 @@ def tile_swintransformerblock_pb_kernel(
             copy_out(t)
             quantise(t)
 
-        for t in range(GROUP):
+        for t in range(HALF):
             prepare(t)
 
         bias_bank = [psum_a.tile([P, BANK], F32, name="bias_bank", tag="product") for h in range(HALVES)]
@@ -244,35 +265,61 @@ def tile_swintransformerblock_pb_kernel(
         nc.vector.tensor_copy(out=bias_all[:, 0:BANK], in_=bias_bank[0][:])
         nc.scalar.copy(out=bias_all[:, BANK:C], in_=bias_bank[1][:])
 
-        for t in range(GROUP, N_TILES):
-            prepare(t)
-
         token_rows_f32 = keep.tile([P, P], F32, name="token_rows_f32")
         token_bank = psum_t.tile([P, P], F32, name="token_bank", tag="transposed")
         token_columns = keep.tile([P, 2 * N_TILES], F32, name="token_columns")
         nc.gpsimd.tensor_copy(out=token_rows_f32[:], in_=token_rows[:])
+        nc.tensor.transpose(token_bank[:], token_rows_f32[:], identity[:])
+        nc.scalar.copy(out=token_columns[:], in_=token_bank[:, 0 : 2 * N_TILES])
+        inverse_scale = keep.tile([P, N_TILES], F32, name="inverse_scale")
+
+        for t in range(HALF, N_TILES):
+            prepare(t)
+
+        nc.vector.reciprocal(out=inverse_scale[:], in_=token_columns[:, 0:N_TILES])
+
+        def measure(t):
+            mean(t)
+            square(t)
+            if t % GROUP == GROUP - 1:
+                root(t - (GROUP - 1))
+
+        def gpsimd_normalises(first):
+            for member in range(first, first + GROUP):
+                if member < GPSIMD_TILES:
+                    normalise(member)
+
+        def scalar_normalises(first):
+            for member in range(first, first + GROUP):
+                if member >= GPSIMD_TILES:
+                    normalise(member)
 
         for t in range(N_TILES):
             project(t)
             add_bias(t, 0)
             if t > 0:
-                mean(t - 1)
-                square(t - 1)
+                measure(t - 1)
+            if t >= 2 * GROUP and t % GROUP == 0:
+                invert(t - 2 * GROUP)
+                gpsimd_normalises(t - 2 * GROUP)
             add_bias(t, 1)
-            if t == GROUP - 1:
-                nc.tensor.transpose(token_bank[:], token_rows_f32[:], identity[:])
-                nc.scalar.copy(out=token_columns[:], in_=token_bank[:, 0 : 2 * N_TILES])
-            if t == GROUP:
-                root(0)
-                nc.gpsimd.tensor_tensor(out=inverse[0][:], in0=padded[:, 0:GROUP], in1=minus_one[:], op=ALU.pow)
-                fold(0, nc.gpsimd)
-        mean(N_TILES - 1)
-        square(N_TILES - 1)
-        root(GROUP)
+            if t >= 2 * GROUP and t % GROUP == 0:
+                fold(t - 2 * GROUP)
+            if t >= 2 * GROUP - 1 and t % GROUP == GROUP - 1:
+                divide(t - (2 * GROUP - 1))
+        measure(N_TILES - 1)
 
-        for t in range(N_TILES):
-            if t == VECTOR_TILES:
-                nc.vector.reciprocal(out=inverse[GROUP][:], in_=padded[:, GROUP:N_TILES])
-                fold(GROUP, nc.vector)
-            normalise(t)
+        scalar_normalises(N_TILES - 3 * GROUP)
+        add_residual_and_store(0)
+        invert(N_TILES - 2 * GROUP)
+        add_residual_and_store(1)
+        fold(N_TILES - 2 * GROUP)
+        scalar_normalises(N_TILES - 2 * GROUP)
+        divide(N_TILES - GROUP)
+        add_residual_and_store(2)
+        invert(N_TILES - GROUP)
+        add_residual_and_store(3)
+        fold(N_TILES - GROUP)
+        scalar_normalises(N_TILES - GROUP)
+        for t in range(4, N_TILES):
             add_residual_and_store(t)

@@ -194,25 +194,28 @@ def tile_swintransformerblock_pb_kernel(
             nc.scalar.activation(out=deviation[:, tiles], in_=sum_squares[:, tiles], func=ACT.Sqrt, scale=1.0 / (C - 1))
 
         def divide(first):
-            tiles = slice(first, first + GROUP)
-            nc.vector.scalar_tensor_tensor(
-                out=divisor[:, tiles],
-                in0=deviation[:, tiles],
-                scalar=EPS,
-                in1=inverse_scale[:, tiles],
-                op0=ALU.add,
-                op1=ALU.mult,
-            )
+            for t in range(first, first + GROUP):
+                nc.vector.tensor_scalar(
+                    out=divisor[:, t : t + 1],
+                    in0=deviation[:, t : t + 1],
+                    scalar1=EPS,
+                    scalar2=inverse_scale[:, t : t + 1],
+                    op0=ALU.add,
+                    op1=ALU.mult,
+                )
 
         def invert(first):
-            tiles = slice(first, first + GROUP)
-            nc.vector.reciprocal(out=gain[:, tiles], in_=divisor[:, tiles])
+            for t in range(first, first + GROUP):
+                nc.vector.reciprocal(out=gain[:, t : t + 1], in_=divisor[:, t : t + 1])
 
         def fold(first):
-            tiles = slice(max(first, GPSIMD_TILES), first + GROUP)
-            if tiles.start < tiles.stop:
-                nc.vector.tensor_tensor(
-                    out=mean_gain[:, tiles], in0=neg_mean[:, tiles], in1=gain[:, tiles], op=ALU.mult
+            for t in range(max(first, GPSIMD_TILES), first + GROUP):
+                nc.vector.tensor_scalar(
+                    out=mean_gain[:, t : t + 1],
+                    in0=neg_mean[:, t : t + 1],
+                    scalar1=gain[:, t : t + 1],
+                    scalar2=None,
+                    op0=ALU.mult,
                 )
 
         def normalise(t):

@@ -58,6 +58,8 @@ def tile_swintransformerblock_pb_kernel(
 
         identity = keep.tile([P, P], F32, name="identity")
         make_identity(nc, identity[:])
+        identity_bf16 = keep.tile([P, P], BF16, name="identity_bf16")
+        make_identity(nc, identity_bf16[:])
 
         nc.scalar.dma_start(out=bias_rows[0:1, :], in_=out_b.rearrange("(o c) -> o c", o=1))
         nc.scalar.dma_start(out=token_rows[0:N_TILES, :], in_=ada1_scale.rearrange("o (t p) i -> (o t) (p i)", p=P))
@@ -112,6 +114,7 @@ def tile_swintransformerblock_pb_kernel(
         product = {}
         biased = [per_tile.tile([P, C], F32, name="biased", tag="biased") for t in range(N_TILES)]
         result = {}
+        x_bank = {}
         sums = keep.tile([P, N_TILES, HALVES], F32, name="sums")
         neg_mean = keep.tile([P, N_TILES], F32, name="neg_mean")
         sum_squares = keep.tile([P, N_TILES], F32, name="sum_squares")
@@ -193,7 +196,18 @@ def tile_swintransformerblock_pb_kernel(
             tiles = slice(first, first + GROUP)
             nc.scalar.activation(out=deviation[:, tiles], in_=sum_squares[:, tiles], func=ACT.Sqrt, scale=1.0 / (C - 1))
 
-        def divide(first):
+        def divide(first, gpsimd_idle=False):
+            tiles = slice(first, first + GROUP)
+            if gpsimd_idle:
+                nc.vector.scalar_tensor_tensor(
+                    out=divisor[:, tiles],
+                    in0=deviation[:, tiles],
+                    scalar=EPS,
+                    in1=inverse_scale[:, tiles],
+                    op0=ALU.add,
+                    op1=ALU.mult,
+                )
+                return
             for t in range(first, first + GROUP):
                 nc.vector.tensor_scalar(
                     out=divisor[:, t : t + 1],
@@ -204,11 +218,19 @@ def tile_swintransformerblock_pb_kernel(
                     op1=ALU.mult,
                 )
 
-        def invert(first):
+        def invert(first, gpsimd_idle=False):
+            tiles = slice(first, first + GROUP)
+            if gpsimd_idle:
+                nc.vector.reciprocal(out=gain[:, tiles], in_=divisor[:, tiles])
+                return
             for t in range(first, first + GROUP):
                 nc.vector.reciprocal(out=gain[:, t : t + 1], in_=divisor[:, t : t + 1])
 
-        def fold(first):
+        def fold(first, gpsimd_idle=False):
+            tiles = slice(first, first + GROUP)
+            if gpsimd_idle:
+                nc.vector.tensor_tensor(out=mean_gain[:, tiles], in0=neg_mean[:, tiles], in1=gain[:, tiles], op=ALU.mult)
+                return
             for t in range(max(first, GPSIMD_TILES), first + GROUP):
                 nc.vector.tensor_scalar(
                     out=mean_gain[:, t : t + 1],
@@ -239,13 +261,13 @@ def tile_swintransformerblock_pb_kernel(
                 )
 
         def add_residual_and_store(t):
-            width = C // (LAST_PIECES if t == N_TILES - 1 else 1)
+            width = C // (LAST_PIECES if t in (0, N_TILES - 1) else 1)
             for c in range(0, C, width):
                 nc.vector.scalar_tensor_tensor(
                     out=result[t][:, c : c + width],
                     in0=result[t][:, c : c + width],
                     scalar=token_columns[:, N_TILES + t : N_TILES + t + 1],
-                    in1=residual[:, t, c : c + width],
+                    in1=x_bank[c // BANK][:] if t == 0 else residual[:, t, c : c + width],
                     op0=ALU.add,
                     op1=ALU.add,
                 )
@@ -303,26 +325,31 @@ def tile_swintransformerblock_pb_kernel(
             if t > 0:
                 measure(t - 1)
             if t >= 2 * GROUP and t % GROUP == 0:
-                invert(t - 2 * GROUP)
+                invert(t - 2 * GROUP, gpsimd_idle=(t == 2 * GROUP))
                 gpsimd_normalises(t - 2 * GROUP)
             add_bias(t, 1)
-            if t >= 2 * GROUP and t % GROUP == 0:
+            if t > 2 * GROUP and t % GROUP == 0:
                 fold(t - 2 * GROUP)
             if t >= 2 * GROUP - 1 and t % GROUP == GROUP - 1:
-                divide(t - (2 * GROUP - 1))
+                divide(t - (2 * GROUP - 1), gpsimd_idle=(t == 2 * GROUP - 1))
+        for h in range(HALVES):
+            x_bank[h] = psum_t.tile([P, BANK], F32, name="x_bank", tag="transposed")
+            nc.tensor.matmul(
+                out=x_bank[h][:], lhsT=identity_bf16[:], rhs=residual[:, 0, BANK * h : BANK * (h + 1)], start=True, stop=True
+            )
         measure(N_TILES - 1)
 
         scalar_normalises(N_TILES - 3 * GROUP)
         add_residual_and_store(0)
-        invert(N_TILES - 2 * GROUP)
+        invert(N_TILES - 2 * GROUP, gpsimd_idle=True)
         add_residual_and_store(1)
-        fold(N_TILES - 2 * GROUP)
+        fold(N_TILES - 2 * GROUP, gpsimd_idle=True)
         scalar_normalises(N_TILES - 2 * GROUP)
-        divide(N_TILES - GROUP)
+        divide(N_TILES - GROUP, gpsimd_idle=True)
         add_residual_and_store(2)
-        invert(N_TILES - GROUP)
+        invert(N_TILES - GROUP, gpsimd_idle=True)
         add_residual_and_store(3)
-        fold(N_TILES - GROUP)
+        fold(N_TILES - GROUP, gpsimd_idle=True)
         scalar_normalises(N_TILES - GROUP)
         for t in range(4, N_TILES):
             add_residual_and_store(t)

@@ -31,7 +31,9 @@ EPS = 1e-5
 HALF = N_TILES // 2
 GROUP = 2
 LAST_PIECES = 2
-GPSIMD_TILES = 3
+GPSIMD_TILES = 4
+GPSIMD_ADDS = (3, 5)
+PSUM_X_TILES = (0, 1, 2, 4, 6)
 
 FLOPS = 2 * TOKENS * C * C
 
@@ -261,17 +263,63 @@ def tile_swintransformerblock_pb_kernel(
                 )
 
         def add_residual_and_store(t):
-            width = C // (LAST_PIECES if t in (0, N_TILES - 1) else 1)
+            width = C // (LAST_PIECES if t in PSUM_X_TILES or t == N_TILES - 1 else 1)
             for c in range(0, C, width):
                 nc.vector.scalar_tensor_tensor(
                     out=result[t][:, c : c + width],
                     in0=result[t][:, c : c + width],
                     scalar=token_columns[:, N_TILES + t : N_TILES + t + 1],
-                    in1=x_bank[c // BANK][:] if t == 0 else residual[:, t, c : c + width],
+                    in1=x_bank[t, c // BANK][:] if t in PSUM_X_TILES else residual[:, t, c : c + width],
                     op0=ALU.add,
                     op1=ALU.add,
                 )
                 nc.sync.dma_start(out=out[0, P * t : P * (t + 1), c : c + width], in_=result[t][:, c : c + width])
+
+        shifted = keep.tile([P, len(GPSIMD_ADDS), C], F32, name="shifted")
+
+        def shift_residual(t):
+            nc.gpsimd.tensor_scalar(
+                out=shifted[:, GPSIMD_ADDS.index(t), :],
+                in0=residual[:, t, :],
+                scalar1=1.0,
+                scalar2=token_columns[:, N_TILES + t : N_TILES + t + 1],
+                op0=ALU.mult,
+                op1=ALU.add,
+            )
+
+        def gpsimd_adds(t):
+            nc.gpsimd.tensor_tensor(
+                out=result[t][:], in0=result[t][:], in1=shifted[:, GPSIMD_ADDS.index(t), :], op=ALU.add
+            )
+
+        def store(t, columns=slice(0, C)):
+            nc.sync.dma_start(out=out[0, P * t : P * (t + 1), columns], in_=result[t][:, columns])
+
+        def add_piece(t, h):
+            half = slice(BANK * h, BANK * (h + 1))
+            nc.vector.scalar_tensor_tensor(
+                out=result[t][:, half],
+                in0=result[t][:, half],
+                scalar=token_columns[:, N_TILES + t : N_TILES + t + 1],
+                in1=x_bank[t, h][:] if t in PSUM_X_TILES else residual[:, t, half],
+                op0=ALU.add,
+                op1=ALU.add,
+            )
+            if t in (0, 1, 2, N_TILES - 1):
+                store(t, half)
+            elif h == HALVES - 1:
+                store(t)
+
+        def x_into_psum(t, pool, tag):
+            for h in range(HALVES):
+                x_bank[t, h] = pool.tile([P, BANK], F32, name="x_bank", tag=tag)
+                nc.tensor.matmul(
+                    out=x_bank[t, h][:],
+                    lhsT=identity_bf16[:],
+                    rhs=residual[:, t, BANK * h : BANK * (h + 1)],
+                    start=True,
+                    stop=True,
+                )
 
         def prepare(t):
             transpose(t)
@@ -324,32 +372,41 @@ def tile_swintransformerblock_pb_kernel(
             add_bias(t, 0)
             if t > 0:
                 measure(t - 1)
+            if t in (2, 3):
+                shift_residual(GPSIMD_ADDS[t - 2])
             if t >= 2 * GROUP and t % GROUP == 0:
                 invert(t - 2 * GROUP, gpsimd_idle=(t == 2 * GROUP))
                 gpsimd_normalises(t - 2 * GROUP)
             add_bias(t, 1)
-            if t > 2 * GROUP and t % GROUP == 0:
-                fold(t - 2 * GROUP)
             if t >= 2 * GROUP - 1 and t % GROUP == GROUP - 1:
-                divide(t - (2 * GROUP - 1), gpsimd_idle=(t == 2 * GROUP - 1))
-        for h in range(HALVES):
-            x_bank[h] = psum_t.tile([P, BANK], F32, name="x_bank", tag="transposed")
-            nc.tensor.matmul(
-                out=x_bank[h][:], lhsT=identity_bf16[:], rhs=residual[:, 0, BANK * h : BANK * (h + 1)], start=True, stop=True
-            )
+                divide(t - (2 * GROUP - 1))
+        x_into_psum(0, psum_t, "transposed")
+        x_into_psum(1, psum_t, "transposed")
+        x_into_psum(2, psum_a, "product")
+        x_into_psum(4, psum_a, "product")
         measure(N_TILES - 1)
 
-        scalar_normalises(N_TILES - 3 * GROUP)
-        add_residual_and_store(0)
-        invert(N_TILES - 2 * GROUP, gpsimd_idle=True)
-        add_residual_and_store(1)
-        fold(N_TILES - 2 * GROUP, gpsimd_idle=True)
-        scalar_normalises(N_TILES - 2 * GROUP)
-        divide(N_TILES - GROUP, gpsimd_idle=True)
-        add_residual_and_store(2)
-        invert(N_TILES - GROUP, gpsimd_idle=True)
-        add_residual_and_store(3)
-        fold(N_TILES - GROUP, gpsimd_idle=True)
-        scalar_normalises(N_TILES - GROUP)
-        for t in range(4, N_TILES):
-            add_residual_and_store(t)
+        invert(4)
+        add_piece(0, 0)
+        fold(4)
+        add_piece(0, 1)
+        scalar_normalises(4)
+        gpsimd_adds(3)
+        x_into_psum(6, psum_t, "transposed")
+        add_piece(1, 0)
+        divide(6)
+        add_piece(1, 1)
+        invert(6)
+        add_piece(2, 0)
+        fold(6)
+        add_piece(2, 1)
+        scalar_normalises(6)
+        gpsimd_adds(5)
+        store(3)
+        add_piece(4, 0)
+        add_piece(4, 1)
+        add_piece(6, 0)
+        add_piece(6, 1)
+        store(5)
+        add_piece(7, 0)
+        add_piece(7, 1)

@@ -32,8 +32,8 @@ HALF = N_TILES // 2
 GROUP = 2
 LAST_PIECES = 2
 GPSIMD_TILES = 4
-GPSIMD_ADDS = (3, 5)
-PSUM_X_TILES = (0, 1, 2, 4, 6)
+GPSIMD_ADDS = (3,)
+PSUM_X_TILES = (0, 1, 2, 4)
 
 FLOPS = 2 * TOKENS * C * C
 
@@ -372,41 +372,38 @@ def tile_swintransformerblock_pb_kernel(
             add_bias(t, 0)
             if t > 0:
                 measure(t - 1)
-            if t in (2, 3):
-                shift_residual(GPSIMD_ADDS[t - 2])
+            if t == 3:
+                shift_residual(GPSIMD_ADDS[0])
             if t >= 2 * GROUP and t % GROUP == 0:
                 invert(t - 2 * GROUP, gpsimd_idle=(t == 2 * GROUP))
                 gpsimd_normalises(t - 2 * GROUP)
             add_bias(t, 1)
-            if t >= 2 * GROUP - 1 and t % GROUP == GROUP - 1:
+            if 2 * GROUP - 1 <= t < N_TILES - 1 and t % GROUP == GROUP - 1:
                 divide(t - (2 * GROUP - 1))
         x_into_psum(0, psum_t, "transposed")
         x_into_psum(1, psum_t, "transposed")
         x_into_psum(2, psum_a, "product")
         x_into_psum(4, psum_a, "product")
-        measure(N_TILES - 1)
 
-        invert(4)
         add_piece(0, 0)
-        fold(4)
+        measure(N_TILES - 1)
         add_piece(0, 1)
-        scalar_normalises(4)
+        divide(4)
         gpsimd_adds(3)
-        x_into_psum(6, psum_t, "transposed")
         add_piece(1, 0)
-        divide(6)
+        invert(4)
         add_piece(1, 1)
-        invert(6)
+        fold(4)
+        scalar_normalises(4)
         add_piece(2, 0)
-        fold(6)
+        divide(6)
         add_piece(2, 1)
-        scalar_normalises(6)
-        gpsimd_adds(5)
+        invert(6)
         store(3)
         add_piece(4, 0)
+        fold(6)
+        scalar_normalises(6)
         add_piece(4, 1)
-        add_piece(6, 0)
-        add_piece(6, 1)
-        store(5)
-        add_piece(7, 0)
-        add_piece(7, 1)
+        for t in range(5, N_TILES):
+            add_piece(t, 0)
+            add_piece(t, 1)

@@ -33,7 +33,7 @@ GROUP = 2
 LAST_PIECES = 2
 GPSIMD_TILES = 4
 GPSIMD_ADDS = (3,)
-PSUM_X_TILES = (0, 1, 2, 4)
+PSUM_X_TILES = (0, 1, 2, 4, 5)
 
 FLOPS = 2 * TOKENS * C * C
 
@@ -86,13 +86,13 @@ def tile_swintransformerblock_pb_kernel(
 
         for t in range(N_TILES):
             load_attention(t)
-        w_words = keep.tile([P, PASSES, 2 * C], U8, name="w_words", align_bytes=64)
-        nc.sync.dma_start(out=w_words[:].bitcast(I32), in_=out_w_words.rearrange("g p b -> p g b").bitcast(I32))
         for quadrant in range(4):
             nc.sync.dma_start(
                 out=w_planes[32 * quadrant : 32 * quadrant + 4, :, :].bitcast(I32),
                 in_=out_w_scales[:, 4 * quadrant : 4 * quadrant + 4, :].rearrange("g r n -> r g n").bitcast(I32),
             )
+        w_words = keep.tile([P, PASSES, 2 * C], U8, name="w_words", align_bytes=64)
+        nc.sync.dma_start(out=w_words[:].bitcast(I32), in_=out_w_words.rearrange("g p b -> p g b").bitcast(I32))
         for t in range(0, N_TILES, 2):
             nc.sync.dma_start(
                 out=residual[:, t : t + 2, :], in_=x[0, P * t : P * (t + 2), :].rearrange("(t p) c -> p t c", p=P)
@@ -384,6 +384,7 @@ def tile_swintransformerblock_pb_kernel(
         x_into_psum(1, psum_t, "transposed")
         x_into_psum(2, psum_a, "product")
         x_into_psum(4, psum_a, "product")
+        x_into_psum(5, psum_t, "transposed")
 
         add_piece(0, 0)
         measure(N_TILES - 1)

from contextlib import ExitStack

import concourse.mybir as mybir
from concourse.masks import make_identity

F32 = mybir.dt.float32
BF16 = mybir.dt.bfloat16
I32 = mybir.dt.int32
U32 = mybir.dt.uint32
U8 = mybir.dt.uint8
FP8X4 = mybir.dt.float8_e4m3fn_x4
FP4X4 = mybir.dt.float4_e2m1fn_x4
ALU = mybir.AluOpType
ACT = mybir.ActivationFunctionType

P = 128
C = 1024
TOKENS = 1024
N_TILES = TOKENS // P
PACK = 4
K_PASS = P * PACK
PASSES = C // K_PASS
BANK = 512
HALVES = C // BANK
WINDOWS_IN_ROW = 4
WINDOW = 8
GRID = 32
SHIFT = 4
ROWS_IN_TILE = P // GRID
EPS = 1e-5
HALF = N_TILES // 2
GROUP = 2
LAST_PIECES = 2
GPSIMD_TILES = 4
GPSIMD_ADDS = (3,)
PSUM_X_TILES = (0, 1, 2, 4, 5)

FLOPS = 2 * TOKENS * C * C


def tile_swintransformerblock_pb_kernel(
    tc, o_attn, out_w_words, out_w_scales, out_b, ada1_scale, ada1_shift, x, out
):
    nc = tc.nc
    with ExitStack() as ctx:
        keep = ctx.enter_context(tc.tile_pool(name="keep", bufs=1))
        per_tile = ctx.enter_context(tc.tile_pool(name="per_tile", bufs=N_TILES))
        psum_t = ctx.enter_context(tc.psum_pool(name="psum_t", bufs=4))
        psum_a = ctx.enter_context(tc.psum_pool(name="psum_a", bufs=4))
        ctx.enter_context(tc.manual_schedule())

        bias_rows = keep.tile([P, C], BF16, name="bias_rows")
        w_planes = keep.tile([P, PASSES, C], U8, name="w_planes", align_bytes=64)
        token_rows = keep.tile([P, P], BF16, name="token_rows")
        ones = keep.tile([P, P], BF16, name="ones")
        nc.vector.memset(bias_rows[:], 0.0)
        nc.vector.memset(w_planes[:].rearrange("p g n -> p (g n)").bitcast(I32), 0)
        nc.vector.memset(token_rows[:], 0.0)
        nc.vector.memset(ones[:], 1.0)

        identity = keep.tile([P, P], F32, name="identity")
        make_identity(nc, identity[:])
        identity_bf16 = keep.tile([P, P], BF16, name="identity_bf16")
        make_identity(nc, identity_bf16[:])

        nc.scalar.dma_start(out=bias_rows[0:1, :], in_=out_b.rearrange("(o c) -> o c", o=1))
        nc.scalar.dma_start(out=token_rows[0:N_TILES, :], in_=ada1_scale.rearrange("o (t p) i -> (o t) (p i)", p=P))
        nc.scalar.dma_start(
            out=token_rows[N_TILES : 2 * N_TILES, :], in_=ada1_shift.rearrange("o (t p) i -> (o t) (p i)", p=P)
        )
        table_warmer = keep.tile([P, 1], F32, name="table_warmer")
        nc.scalar.activation(out=table_warmer[:], in_=ones[:, 0:1], func=ACT.Sqrt)

        attention = [per_tile.tile([P, C], BF16, name="attention", tag="attention") for t in range(N_TILES)]
        residual = keep.tile([P, N_TILES, C], BF16, name="residual")

        def load_attention(t):
            band, window_row = divmod((ROWS_IN_TILE * t - SHIFT) % GRID, WINDOW)
            places = WINDOW * window_row
            nc.sync.dma_start(
                out=attention[t][:],
                in_=o_attn[
                    WINDOWS_IN_ROW * band : WINDOWS_IN_ROW * (band + 1), places : places + ROWS_IN_TILE * WINDOW, :
                ].rearrange("w q c -> q w c"),
            )

        for t in range(N_TILES):
            load_attention(t)
        for quadrant in range(4):
            nc.sync.dma_start(
                out=w_planes[32 * quadrant : 32 * quadrant + 4, :, :].bitcast(I32),
                in_=out_w_scales[:, 4 * quadrant : 4 * quadrant + 4, :].rearrange("g r n -> r g n").bitcast(I32),
            )
        w_words = keep.tile([P, PASSES, 2 * C], U8, name="w_words", align_bytes=64)
        nc.sync.dma_start(out=w_words[:].bitcast(I32), in_=out_w_words.rearrange("g p b -> p g b").bitcast(I32))
        for t in range(0, N_TILES, 2):
            nc.sync.dma_start(
                out=residual[:, t : t + 2, :], in_=x[0, P * t : P * (t + 2), :].rearrange("(t p) c -> p t c", p=P)
            )

        permutation = keep.tile([P, P], F32, name="permutation")
        from_partition = identity[:].rearrange("p (d c w) -> p d w c", d=ROWS_IN_TILE, c=WINDOW, w=WINDOWS_IN_ROW)
        to_column = permutation[:].rearrange("p (d j) -> p d j", d=ROWS_IN_TILE)
        last = WINDOWS_IN_ROW - 1
        nc.vector.tensor_copy(
            out=to_column[:, :, SHIFT : SHIFT + last * WINDOW].rearrange("p d (w c) -> p d w c", w=last),
            in_=from_partition[:, :, 0:last, :],
        )
        nc.vector.tensor_copy(out=to_column[:, :, GRID - SHIFT : GRID], in_=from_partition[:, :, last, 0:SHIFT])
        nc.vector.tensor_copy(out=to_column[:, :, 0:SHIFT], in_=from_partition[:, :, last, SHIFT:WINDOW])

        transposed = {}
        grouped = {}
        codes = {}
        planes = {}
        product = {}
        biased = [per_tile.tile([P, C], F32, name="biased", tag="biased") for t in range(N_TILES)]
        result = {}
        x_bank = {}
        sums = keep.tile([P, N_TILES, HALVES], F32, name="sums")
        neg_mean = keep.tile([P, N_TILES], F32, name="neg_mean")
        sum_squares = keep.tile([P, N_TILES], F32, name="sum_squares")
        deviation = keep.tile([P, N_TILES], F32, name="deviation")
        divisor = keep.tile([P, N_TILES], F32, name="divisor")
        gain = keep.tile([P, N_TILES], F32, name="gain")
        mean_gain = keep.tile([P, N_TILES], F32, name="mean_gain")

        def transpose(t):
            transposed[t] = psum_t.tile([P, PASSES, 2, P], F32, name="transposed", tag="transposed")
            pairs = attention[t][:].bitcast(F32)
            for g in range(PASSES):
                for u in range(2):
                    nc.tensor.transpose(
                        transposed[t][:, g, u, :],
                        pairs[:, (K_PASS // 2) * g + u : (K_PASS // 2) * (g + 1) : 2],
                        permutation[:],
                    )

        def copy_out(t):
            grouped[t] = per_tile.tile([P, PASSES, P, PACK], BF16, name="grouped", tag="grouped", align_bytes=64)
            nc.scalar.copy(out=grouped[t][:].bitcast(F32), in_=transposed[t][:].rearrange("p g u m -> p g m u"))

        def quantise(t):
            codes[t] = per_tile.tile([P, PASSES * P], U32, name="codes", tag="codes", align_bytes=64)
            planes[t] = per_tile.tile([P, PASSES * P], U8, name="planes", tag="planes", align_bytes=64)
            nc.vector.quantize_mx(
                out=codes[t][:].bitcast(FP8X4),
                scales=planes[t][:],
                in_=grouped[t][:].rearrange("p g m i -> p (g m i)"),
            )

        def project(t):
            for h in range(HALVES):
                product[t, h] = psum_a.tile([P, BANK], F32, name="product", tag="product")
                for g in range(PASSES):
                    nc.tensor.matmul_mx(
                        out=product[t, h][:],
                        lhsT=codes[t][:, P * g : P * (g + 1)].bitcast(FP8X4),
                        lhsT_scale=planes[t][:, P * g : P * (g + 1)],
                        rhs=w_words[:, g, 2 * BANK * h : 2 * BANK * (h + 1)].bitcast(FP4X4),
                        rhs_scale=w_planes[:, g, BANK * h : BANK * (h + 1)],
                        start=(g == 0),
                        stop=(g == PASSES - 1),
                    )

        def add_bias(t, h):
            nc.vector.scalar_tensor_tensor(
                out=biased[t][:, BANK * h : BANK * (h + 1)],
                in0=product[t, h][:],
                scalar=1.0,
                in1=bias_all[:, BANK * h : BANK * (h + 1)],
                op0=ALU.mult,
                op1=ALU.add,
                accum_out=sums[:, t, h : h + 1],
            )

        def mean(t):
            nc.vector.tensor_scalar(
                out=neg_mean[:, t : t + 1],
                in0=sums[:, t, 0:1],
                scalar1=sums[:, t, 1:2],
                scalar2=-1.0 / C,
                op0=ALU.add,
                op1=ALU.mult,
            )

        def square(t):
            squares = per_tile.tile([P, C], BF16, name="squares", tag="squares")
            nc.scalar.activation(
                out=squares[:],
                in_=biased[t][:],
                func=ACT.Square,
                bias=neg_mean[:, t : t + 1],
                accum_out=sum_squares[:, t : t + 1],
            )

        def root(first):
            tiles = slice(first, first + GROUP)
            nc.scalar.activation(out=deviation[:, tiles], in_=sum_squares[:, tiles], func=ACT.Sqrt, scale=1.0 / (C - 1))

        def divide(first, gpsimd_idle=False):
            tiles = slice(first, first + GROUP)
            if gpsimd_idle:
                nc.vector.scalar_tensor_tensor(
                    out=divisor[:, tiles],
                    in0=deviation[:, tiles],
                    scalar=EPS,
                    in1=inverse_scale[:, tiles],
                    op0=ALU.add,
                    op1=ALU.mult,
                )
                return
            for t in range(first, first + GROUP):
                nc.vector.tensor_scalar(
                    out=divisor[:, t : t + 1],
                    in0=deviation[:, t : t + 1],
                    scalar1=EPS,
                    scalar2=inverse_scale[:, t : t + 1],
                    op0=ALU.add,
                    op1=ALU.mult,
                )

        def invert(first, gpsimd_idle=False):
            tiles = slice(first, first + GROUP)
            if gpsimd_idle:
                nc.vector.reciprocal(out=gain[:, tiles], in_=divisor[:, tiles])
                return
            for t in range(first, first + GROUP):
                nc.vector.reciprocal(out=gain[:, t : t + 1], in_=divisor[:, t : t + 1])

        def fold(first, gpsimd_idle=False):
            tiles = slice(first, first + GROUP)
            if gpsimd_idle:
                nc.vector.tensor_tensor(out=mean_gain[:, tiles], in0=neg_mean[:, tiles], in1=gain[:, tiles], op=ALU.mult)
                return
            for t in range(max(first, GPSIMD_TILES), first + GROUP):
                nc.vector.tensor_scalar(
                    out=mean_gain[:, t : t + 1],
                    in0=neg_mean[:, t : t + 1],
                    scalar1=gain[:, t : t + 1],
                    scalar2=None,
                    op0=ALU.mult,
                )

        def normalise(t):
            result[t] = per_tile.tile([P, C], F32, name="result", tag="result")
            if t < GPSIMD_TILES:
                nc.gpsimd.tensor_scalar(
                    out=result[t][:],
                    in0=biased[t][:],
                    scalar1=neg_mean[:, t : t + 1],
                    scalar2=gain[:, t : t + 1],
                    op0=ALU.add,
                    op1=ALU.mult,
                )
            else:
                nc.scalar.activation(
                    out=result[t][:],
                    in_=biased[t][:],
                    func=ACT.Identity,
                    scale=gain[:, t : t + 1],
                    bias=mean_gain[:, t : t + 1],
                )

        def add_residual_and_store(t):
            width = C // (LAST_PIECES if t in PSUM_X_TILES or t == N_TILES - 1 else 1)
            for c in range(0, C, width):
                nc.vector.scalar_tensor_tensor(
                    out=result[t][:, c : c + width],
                    in0=result[t][:, c : c + width],
                    scalar=token_columns[:, N_TILES + t : N_TILES + t + 1],
                    in1=x_bank[t, c // BANK][:] if t in PSUM_X_TILES else residual[:, t, c : c + width],
                    op0=ALU.add,
                    op1=ALU.add,
                )
                nc.sync.dma_start(out=out[0, P * t : P * (t + 1), c : c + width], in_=result[t][:, c : c + width])

        shifted = keep.tile([P, len(GPSIMD_ADDS), C], F32, name="shifted")

        def shift_residual(t):
            nc.gpsimd.tensor_scalar(
                out=shifted[:, GPSIMD_ADDS.index(t), :],
                in0=residual[:, t, :],
                scalar1=1.0,
                scalar2=token_columns[:, N_TILES + t : N_TILES + t + 1],
                op0=ALU.mult,
                op1=ALU.add,
            )

        def gpsimd_adds(t):
            nc.gpsimd.tensor_tensor(
                out=result[t][:], in0=result[t][:], in1=shifted[:, GPSIMD_ADDS.index(t), :], op=ALU.add
            )

        def store(t, columns=slice(0, C)):
            nc.sync.dma_start(out=out[0, P * t : P * (t + 1), columns], in_=result[t][:, columns])

        def add_piece(t, h):
            half = slice(BANK * h, BANK * (h + 1))
            nc.vector.scalar_tensor_tensor(
                out=result[t][:, half],
                in0=result[t][:, half],
                scalar=token_columns[:, N_TILES + t : N_TILES + t + 1],
                in1=x_bank[t, h][:] if t in PSUM_X_TILES else residual[:, t, half],
                op0=ALU.add,
                op1=ALU.add,
            )
            if t in (0, 1, 2, N_TILES - 1):
                store(t, half)
            elif h == HALVES - 1:
                store(t)

        def x_into_psum(t, pool, tag):
            for h in range(HALVES):
                x_bank[t, h] = pool.tile([P, BANK], F32, name="x_bank", tag=tag)
                nc.tensor.matmul(
                    out=x_bank[t, h][:],
                    lhsT=identity_bf16[:],
                    rhs=residual[:, t, BANK * h : BANK * (h + 1)],
                    start=True,
                    stop=True,
                )

        def prepare(t):
            transpose(t)
            copy_out(t)
            quantise(t)

        for t in range(HALF):
            prepare(t)

        bias_bank = [psum_a.tile([P, BANK], F32, name="bias_bank", tag="product") for h in range(HALVES)]
        bias_all = keep.tile([P, C], F32, name="bias_all")
        for h in range(HALVES):
            nc.tensor.matmul(
                out=bias_bank[h][:], lhsT=ones[:], rhs=bias_rows[:, BANK * h : BANK * (h + 1)], start=True, stop=True
            )
        nc.vector.tensor_copy(out=bias_all[:, 0:BANK], in_=bias_bank[0][:])
        nc.scalar.copy(out=bias_all[:, BANK:C], in_=bias_bank[1][:])

        token_rows_f32 = keep.tile([P, P], F32, name="token_rows_f32")
        token_bank = psum_t.tile([P, P], F32, name="token_bank", tag="transposed")
        token_columns = keep.tile([P, 2 * N_TILES], F32, name="token_columns")
        nc.gpsimd.tensor_copy(out=token_rows_f32[:], in_=token_rows[:])
        nc.tensor.transpose(token_bank[:], token_rows_f32[:], identity[:])
        nc.scalar.copy(out=token_columns[:], in_=token_bank[:, 0 : 2 * N_TILES])
        inverse_scale = keep.tile([P, N_TILES], F32, name="inverse_scale")

        for t in range(HALF, N_TILES):
            prepare(t)

        nc.vector.reciprocal(out=inverse_scale[:], in_=token_columns[:, 0:N_TILES])

        def measure(t):
            mean(t)
            square(t)
            if t % GROUP == GROUP - 1:
                root(t - (GROUP - 1))

        def gpsimd_normalises(first):
            for member in range(first, first + GROUP):
                if member < GPSIMD_TILES:
                    normalise(member)

        def scalar_normalises(first):
            for member in range(first, first + GROUP):
                if member >= GPSIMD_TILES:
                    normalise(member)

        for t in range(N_TILES):
            project(t)
            add_bias(t, 0)
            if t > 0:
                measure(t - 1)
            if t == 3:
                shift_residual(GPSIMD_ADDS[0])
            if t >= 2 * GROUP and t % GROUP == 0:
                invert(t - 2 * GROUP, gpsimd_idle=(t == 2 * GROUP))
                gpsimd_normalises(t - 2 * GROUP)
            add_bias(t, 1)
            if 2 * GROUP - 1 <= t < N_TILES - 1 and t % GROUP == GROUP - 1:
                divide(t - (2 * GROUP - 1))
        x_into_psum(0, psum_t, "transposed")
        x_into_psum(1, psum_t, "transposed")
        x_into_psum(2, psum_a, "product")
        x_into_psum(4, psum_a, "product")
        x_into_psum(5, psum_t, "transposed")

        add_piece(0, 0)
        measure(N_TILES - 1)
        add_piece(0, 1)
        divide(4)
        gpsimd_adds(3)
        add_piece(1, 0)
        invert(4)
        add_piece(1, 1)
        fold(4)
        scalar_normalises(4)
        add_piece(2, 0)
        divide(6)
        add_piece(2, 1)
        invert(6)
        store(3)
        add_piece(4, 0)
        fold(6)
        scalar_normalises(6)
        add_piece(4, 1)
        for t in range(5, N_TILES):
            add_piece(t, 0)
            add_piece(t, 1)
